import numpy as np
import ml_dtypes


def mxq(x, axis, fmt="e4m3"):
    dtype, down = {"e4m3": (ml_dtypes.float8_e4m3fn, 7), "e5m2": (ml_dtypes.float8_e5m2, 14)}[fmt]
    v = np.moveaxis(np.asarray(x, np.float32).astype(ml_dtypes.bfloat16).astype(np.float64), axis, -1)
    blocks = v.reshape(v.shape[:-1] + (-1, 32))
    amax = np.abs(blocks).max(-1, keepdims=True)
    byte = np.maximum(np.where(amax > 0, np.frexp(amax)[1] - 1 + 127, 0) - down, 1)
    scale = np.exp2(byte - 127.0)
    codes = (blocks / scale).astype(np.float32).astype(dtype).astype(np.float64)
    return np.moveaxis((codes * scale).reshape(v.shape), -1, axis)


WIDE = False


def mx_kscale(k):
    if not WIDE:
        return np.ones(k)
    levels = np.array([20, -20, 10, -10, 0])
    a = np.random.permutation(np.resize(levels, k // 512 * 4)).reshape(k // 512, 4)
    idx = np.arange(k)
    return np.exp2(a[idx // 512, idx % 128 // 32])


BF16 = ml_dtypes.bfloat16


def bf(x):
    return np.asarray(x, np.float32).astype(BF16)


def f64(x):
    return np.asarray(x).astype(np.float64)


B, T, N, C, WIN, F = 1, 4, 512, 512, 3, 3
NW = T - WIN + 1


def sigmoid(v):
    return 1.0 / (1.0 + np.exp(-v))


def setup_inputs():
    s = mx_kscale(B * N).reshape(B, 1, N, 1)
    agg0 = bf(np.random.standard_normal((B, NW, N, C)))
    W = bf(np.random.standard_normal((NW, F, C, 2 * C)) / np.sqrt(C))
    b = bf(np.random.standard_normal((NW, F, 2 * C)) * 0.3)
    g = bf(np.random.standard_normal((B, NW, N, C)) * np.exp2(np.random.randint(-12, 1, (B, NW, N, 1))) / s)
    pre = f64(agg0)[:, :, None] @ f64(W) + f64(b)[None, :, :, None, :]
    return {"agg": bf(f64(agg0) * s), "W": W, "b": b, "pre": np.asarray(pre, np.float32), "grad_out": g}


def reference(agg, W, b, pre, grad_out):
    p = f64(pre)
    lhs, rhs = p[..., :C], p[..., C:]
    sg = sigmoid(rhs)
    glu = lhs * sg
    top = glu.max(axis=2, keepdims=True)
    hit = (glu == top) * 1.0
    share = hit / hit.sum(axis=2, keepdims=True)
    dglu = f64(grad_out)[:, :, None] * share
    dpre = np.concatenate([dglu * sg, dglu * lhs * sg * (1.0 - sg)], axis=-1)
    a = mxq(f64(agg).transpose(1, 0, 2, 3).reshape(NW, B * N, C), 1, "e4m3")
    d = mxq(dpre.transpose(1, 2, 0, 3, 4).reshape(NW, F, B * N, 2 * C), 2, "e5m2")
    return a.transpose(0, 2, 1)[:, None] @ d

@@ -1,0 +1,189 @@
+from contextlib import ExitStack
+
+import concourse.mybir as mybir
+
+F32 = mybir.dt.float32
+BF16 = mybir.dt.bfloat16
+U32 = mybir.dt.uint32
+U8 = mybir.dt.uint8
+E4M3_X4 = mybir.dt.float8_e4m3fn_x4
+E5M2_X4 = mybir.dt.float8_e5m2_x4
+ALU = mybir.AluOpType
+ACT = mybir.ActivationFunctionType
+
+P = 128
+PACK = 4
+WINDOWS = 2
+BRANCHES = 3
+NODES = P * PACK
+CHANNELS = 512
+BLOCK = 256
+BLOCKS = CHANNELS // BLOCK
+N_PASS = 2 * BLOCK
+M_TILE = 128
+M_TILES = CHANNELS // M_TILE
+RUN = 4
+
+FLOPS = 2 * WINDOWS * BRANCHES * NODES * CHANNELS * 2 * CHANNELS
+BYTES = WINDOWS * NODES * CHANNELS * (2 + 2) + 2 * WINDOWS * BRANCHES * NODES * 2 * CHANNELS * 4
+
+TIE_SLOPE = 0.25
+TIE_SHIFT = -0.75
+TIE_OFFSET = 0.125
+SHARE_SCALE = 8.0 / 3.0
+
+
+def rows_to_words(engine_copy, grouped, rows):
+    engine_copy(
+        out=grouped.rearrange("p (c i) j -> p c j i", i=RUN),
+        in_=rows.rearrange("p j (c i) -> p c j i", i=RUN),
+    )
+
+
+def tile_stsindividuallayer_pb_v_kernel(tc, agg, W, b, pre, grad_out, out):
+    nc = tc.nc
+    with ExitStack() as ctx:
+        keep = ctx.enter_context(tc.tile_pool(name="keep", bufs=1))
+        slabs = ctx.enter_context(tc.tile_pool(name="slabs", bufs=WINDOWS * BLOCKS))
+        once = ctx.enter_context(tc.tile_pool(name="once", bufs=1))
+        twice = ctx.enter_context(tc.tile_pool(name="twice", bufs=2))
+        branch = ctx.enter_context(tc.tile_pool(name="branch", bufs=3))
+        stage = ctx.enter_context(tc.tile_pool(name="stage", bufs=8))
+        psum = ctx.enter_context(tc.psum_pool(name="psum", bufs=8))
+
+        agg_rows = keep.tile([P, WINDOWS, PACK, CHANNELS], BF16)
+        grad_rows = keep.tile([P, WINDOWS, PACK, CHANNELS], BF16)
+        agg_codes = keep.tile([P, WINDOWS, CHANNELS], U32, align_bytes=64)
+        agg_scales = keep.tile([P, WINDOWS, CHANNELS], U8, align_bytes=64)
+
+        for w in range(WINDOWS):
+            nc.sync.dma_start(
+                out=agg_rows[:, w], in_=agg[0, w].rearrange("(p j) c -> p j c", j=PACK)
+            )
+            agg_grouped = once.tile([P, CHANNELS, PACK], BF16, align_bytes=64)
+            rows_to_words(nc.vector.tensor_copy, agg_grouped[:], agg_rows[:, w])
+            nc.vector.quantize_mx(
+                out=agg_codes[:, w].bitcast(E4M3_X4),
+                scales=agg_scales[:, w],
+                in_=agg_grouped[:].rearrange("p c j -> p (c j)"),
+            )
+
+            for blk in range(BLOCKS):
+                c0 = blk * BLOCK
+                lhs = slabs.tile([P, BRANCHES, PACK, BLOCK], F32)
+                rhs = slabs.tile([P, BRANCHES, PACK, BLOCK], F32)
+                for f in range(BRANCHES):
+                    pre_rows = pre[0, w, f].rearrange("(p j) n -> p j n", j=PACK)
+                    nc.sync.dma_start(
+                        out=rhs[:, f], in_=pre_rows[:, :, CHANNELS + c0 : CHANNELS + c0 + BLOCK]
+                    )
+                    nc.sync.dma_start(out=lhs[:, f], in_=pre_rows[:, :, c0 : c0 + BLOCK])
+                if blk == 0:
+                    nc.sync.dma_start(
+                        out=grad_rows[:, w],
+                        in_=grad_out[0, w].rearrange("(p j) c -> p j c", j=PACK),
+                    )
+
+                sg = rhs
+                glu = lhs
+                for f in range(BRANCHES):
+                    nc.scalar.activation(out=sg[:, f], in_=rhs[:, f], func=ACT.Sigmoid)
+                    nc.vector.tensor_tensor(
+                        out=glu[:, f], in0=lhs[:, f], in1=sg[:, f], op=ALU.mult
+                    )
+
+                top01 = once.tile([P, PACK, BLOCK], F32)
+                nc.vector.tensor_tensor(out=top01[:], in0=glu[:, 0], in1=glu[:, 1], op=ALU.max)
+                top = twice.tile([P, PACK, BLOCK], F32)
+                nc.vector.tensor_tensor(out=top[:], in0=top01[:], in1=glu[:, 2], op=ALU.max)
+                hit = twice.tile([P, BRANCHES, PACK, BLOCK], BF16)
+                nc.vector.tensor_tensor(
+                    out=hit[:],
+                    in0=glu[:],
+                    in1=top[:].unsqueeze(1).to_broadcast([P, BRANCHES, PACK, BLOCK]),
+                    op=ALU.is_equal,
+                )
+                hits01 = once.tile([P, PACK, BLOCK], BF16)
+                nc.vector.tensor_tensor(out=hits01[:], in0=hit[:, 0], in1=hit[:, 1], op=ALU.add)
+                tied = twice.tile([P, PACK, BLOCK], BF16)
+                nc.vector.tensor_tensor(out=tied[:], in0=hits01[:], in1=hit[:, 2], op=ALU.add)
+
+                tie_square = twice.tile([P, PACK, BLOCK], BF16)
+                nc.scalar.activation(
+                    out=tie_square[:], in_=tied[:], func=ACT.Square, bias=TIE_SHIFT, scale=TIE_SLOPE
+                )
+                grad_share = once.tile([P, PACK, BLOCK], F32)
+                nc.vector.scalar_tensor_tensor(
+                    out=grad_share[:],
+                    in0=tie_square[:],
+                    scalar=TIE_OFFSET,
+                    in1=grad_rows[:, w, :, c0 : c0 + BLOCK],
+                    op0=ALU.add,
+                    op1=ALU.mult,
+                )
+                neg_grad_top = once.tile([P, PACK, BLOCK], F32)
+                nc.vector.scalar_tensor_tensor(
+                    out=neg_grad_top[:],
+                    in0=grad_share[:],
+                    scalar=-SHARE_SCALE,
+                    in1=top[:],
+                    op0=ALU.mult,
+                    op1=ALU.mult,
+                )
+
+                for f in range(BRANCHES):
+                    dpre = branch.tile([P, PACK, N_PASS], BF16)
+                    nc.vector.scalar_tensor_tensor(
+                        out=dpre[:, :, 0:BLOCK],
+                        in0=sg[:, f],
+                        scalar=SHARE_SCALE,
+                        in1=grad_share[:],
+                        op0=ALU.mult,
+                        op1=ALU.mult,
+                    )
+                    nc.vector.scalar_tensor_tensor(
+                        out=dpre[:, :, BLOCK:N_PASS],
+                        in0=sg[:, f],
+                        scalar=1.0,
+                        in1=neg_grad_top[:],
+                        op0=ALU.subtract,
+                        op1=ALU.mult,
+                    )
+                    halves = dpre[:].rearrange("p j (h c) -> p j h c", h=2)
+                    nc.vector.tensor_tensor(
+                        out=halves,
+                        in0=halves,
+                        in1=hit[:, f].unsqueeze(2).to_broadcast([P, PACK, 2, BLOCK]),
+                        op=ALU.mult,
+                    )
+
+                    grouped = branch.tile([P, N_PASS, PACK], BF16, align_bytes=64)
+                    rows_to_words(nc.scalar.copy, grouped[:], dpre[:])
+                    codes = branch.tile([P, N_PASS], U32, align_bytes=64)
+                    scales = branch.tile([P, N_PASS], U8, align_bytes=64)
+                    nc.vector.quantize_mx(
+                        out=codes[:].bitcast(E5M2_X4),
+                        scales=scales[:],
+                        in_=grouped[:].rearrange("p n j -> p (n j)"),
+                    )
+
+                    for m in range(M_TILES):
+                        m_cols = slice(m * M_TILE, (m + 1) * M_TILE)
+                        acc = psum.tile([M_TILE, N_PASS], F32)
+                        nc.tensor.matmul_mx(
+                            out=acc[:],
+                            lhsT=agg_codes[:, w, m_cols].bitcast(E4M3_X4),
+                            lhsT_scale=agg_scales[:, w, m_cols],
+                            rhs=codes[:].bitcast(E5M2_X4),
+                            rhs_scale=scales[:],
+                            start=True,
+                            stop=True,
+                        )
+                        result = stage.tile([M_TILE, N_PASS], F32)
+                        nc.scalar.copy(out=result[:], in_=acc[:])
+                        nc.sync.dma_start(
+                            out=out[w, f, m_cols, :].rearrange("p (h c) -> p h c", h=2)[
+                                :, :, c0 : c0 + BLOCK
+                            ],
+                            in_=result[:].rearrange("p (h c) -> p h c", h=2),
+                        )

@@ -19,6 +19,7 @@ NODES = P * PACK
 CHANNELS = 512
 BLOCK = 256
 BLOCKS = CHANNELS // BLOCK
+SLABS = WINDOWS * BLOCKS
 N_PASS = 2 * BLOCK
 M_TILE = 128
 M_TILES = CHANNELS // M_TILE
@@ -33,18 +34,25 @@ TIE_OFFSET = 0.125
 SHARE_SCALE = 8.0 / 3.0
 
 
-def rows_to_words(engine_copy, grouped, rows):
-    engine_copy(
-        out=grouped.rearrange("p (c i) j -> p c j i", i=RUN),
-        in_=rows.rearrange("p j (c i) -> p c j i", i=RUN),
-    )
+def rows_in_runs(rows):
+    return rows.rearrange("p j (c i) -> p c j i", i=RUN)
+
+
+def words_in_runs(words):
+    return words.rearrange("p (c i) j -> p c j i", i=RUN)
+
+
+def flat(words):
+    return words.rearrange("p c j -> p (c j)")
 
 
 def tile_stsindividuallayer_pb_v_kernel(tc, agg, W, b, pre, grad_out, out):
     nc = tc.nc
     with ExitStack() as ctx:
         keep = ctx.enter_context(tc.tile_pool(name="keep", bufs=1))
-        slabs = ctx.enter_context(tc.tile_pool(name="slabs", bufs=WINDOWS * BLOCKS))
+        raw = ctx.enter_context(tc.tile_pool(name="raw", bufs=BRANCHES))
+        words = ctx.enter_context(tc.tile_pool(name="words", bufs=3 * BRANCHES))
+        flags = ctx.enter_context(tc.tile_pool(name="flags", bufs=2 * BRANCHES))
         once = ctx.enter_context(tc.tile_pool(name="once", bufs=1))
         twice = ctx.enter_context(tc.tile_pool(name="twice", bufs=2))
         branch = ctx.enter_context(tc.tile_pool(name="branch", bufs=3))
@@ -53,137 +61,194 @@ def tile_stsindividuallayer_pb_v_kernel(tc, agg, W, b, pre, grad_out, out):
 
         agg_rows = keep.tile([P, WINDOWS, PACK, CHANNELS], BF16)
         grad_rows = keep.tile([P, WINDOWS, PACK, CHANNELS], BF16)
+        grad_words = keep.tile([P, WINDOWS, CHANNELS, PACK], BF16)
         agg_codes = keep.tile([P, WINDOWS, CHANNELS], U32, align_bytes=64)
         agg_scales = keep.tile([P, WINDOWS, CHANNELS], U8, align_bytes=64)
 
-        for w in range(WINDOWS):
+        rhs_rows_of = {}
+        lhs_rows_of = {}
+        sg_of = {}
+        glu_of = {}
+        hit_of = {}
+        top_of = {}
+        tie_square_of = {}
+        dpre_of = {}
+
+        def load_window(w):
+            nc.sync.dma_start(
+                out=grad_rows[:, w], in_=grad_out[0, w].rearrange("(p j) c -> p j c", j=PACK)
+            )
             nc.sync.dma_start(
                 out=agg_rows[:, w], in_=agg[0, w].rearrange("(p j) c -> p j c", j=PACK)
             )
-            agg_grouped = once.tile([P, CHANNELS, PACK], BF16, align_bytes=64)
-            rows_to_words(nc.vector.tensor_copy, agg_grouped[:], agg_rows[:, w])
+
+        def prepare_window(w):
+            nc.scalar.copy(out=words_in_runs(grad_words[:, w]), in_=rows_in_runs(grad_rows[:, w]))
+            agg_words = once.tile([P, CHANNELS, PACK], BF16, align_bytes=64)
+            nc.scalar.copy(out=words_in_runs(agg_words[:]), in_=rows_in_runs(agg_rows[:, w]))
             nc.vector.quantize_mx(
                 out=agg_codes[:, w].bitcast(E4M3_X4),
                 scales=agg_scales[:, w],
-                in_=agg_grouped[:].rearrange("p c j -> p (c j)"),
+                in_=flat(agg_words[:]),
             )
 
-            for blk in range(BLOCKS):
-                c0 = blk * BLOCK
-                lhs = slabs.tile([P, BRANCHES, PACK, BLOCK], F32)
-                rhs = slabs.tile([P, BRANCHES, PACK, BLOCK], F32)
-                for f in range(BRANCHES):
-                    pre_rows = pre[0, w, f].rearrange("(p j) n -> p j n", j=PACK)
-                    nc.sync.dma_start(
-                        out=rhs[:, f], in_=pre_rows[:, :, CHANNELS + c0 : CHANNELS + c0 + BLOCK]
-                    )
-                    nc.sync.dma_start(out=lhs[:, f], in_=pre_rows[:, :, c0 : c0 + BLOCK])
-                if blk == 0:
-                    nc.sync.dma_start(
-                        out=grad_rows[:, w],
-                        in_=grad_out[0, w].rearrange("(p j) c -> p j c", j=PACK),
-                    )
+        def load(s, f):
+            w, c0 = s // BLOCKS, (s % BLOCKS) * BLOCK
+            pre_rows = pre[0, w, f].rearrange("(p j) n -> p j n", j=PACK)
+            rhs_rows = raw.tile([P, PACK, BLOCK], F32)
+            nc.sync.dma_start(
+                out=rhs_rows[:], in_=pre_rows[:, :, CHANNELS + c0 : CHANNELS + c0 + BLOCK]
+            )
+            lhs_rows = raw.tile([P, PACK, BLOCK], F32)
+            nc.sync.dma_start(out=lhs_rows[:], in_=pre_rows[:, :, c0 : c0 + BLOCK])
+            rhs_rows_of[s, f] = rhs_rows
+            lhs_rows_of[s, f] = lhs_rows
 
-                sg = rhs
-                glu = lhs
-                for f in range(BRANCHES):
-                    nc.scalar.activation(out=sg[:, f], in_=rhs[:, f], func=ACT.Sigmoid)
-                    nc.vector.tensor_tensor(
-                        out=glu[:, f], in0=lhs[:, f], in1=sg[:, f], op=ALU.mult
-                    )
+        def convert(s, f):
+            sg = words.tile([P, BLOCK, PACK], F32)
+            nc.scalar.activation(
+                out=words_in_runs(sg[:]), in_=rows_in_runs(rhs_rows_of[s, f][:]), func=ACT.Sigmoid
+            )
+            glu = words.tile([P, BLOCK, PACK], F32)
+            nc.scalar.copy(out=words_in_runs(glu[:]), in_=rows_in_runs(lhs_rows_of[s, f][:]))
+            sg_of[s, f] = sg
+            glu_of[s, f] = glu
 
-                top01 = once.tile([P, PACK, BLOCK], F32)
-                nc.vector.tensor_tensor(out=top01[:], in0=glu[:, 0], in1=glu[:, 1], op=ALU.max)
-                top = twice.tile([P, PACK, BLOCK], F32)
-                nc.vector.tensor_tensor(out=top[:], in0=top01[:], in1=glu[:, 2], op=ALU.max)
-                hit = twice.tile([P, BRANCHES, PACK, BLOCK], BF16)
+        def gate_products(s):
+            for f in range(BRANCHES):
+                glu = glu_of[s, f]
+                nc.vector.tensor_tensor(out=glu[:], in0=glu[:], in1=sg_of[s, f][:], op=ALU.mult)
+
+        def winners(s):
+            top01 = once.tile([P, BLOCK, PACK], F32)
+            nc.vector.tensor_tensor(
+                out=top01[:], in0=glu_of[s, 0][:], in1=glu_of[s, 1][:], op=ALU.max
+            )
+            top = twice.tile([P, BLOCK, PACK], F32)
+            nc.vector.tensor_tensor(out=top[:], in0=top01[:], in1=glu_of[s, 2][:], op=ALU.max)
+            for f in range(BRANCHES):
+                hit = flags.tile([P, BLOCK, PACK], BF16)
                 nc.vector.tensor_tensor(
-                    out=hit[:],
-                    in0=glu[:],
-                    in1=top[:].unsqueeze(1).to_broadcast([P, BRANCHES, PACK, BLOCK]),
-                    op=ALU.is_equal,
+                    out=hit[:], in0=glu_of[s, f][:], in1=top[:], op=ALU.is_equal
                 )
-                hits01 = once.tile([P, PACK, BLOCK], BF16)
-                nc.vector.tensor_tensor(out=hits01[:], in0=hit[:, 0], in1=hit[:, 1], op=ALU.add)
-                tied = twice.tile([P, PACK, BLOCK], BF16)
-                nc.vector.tensor_tensor(out=tied[:], in0=hits01[:], in1=hit[:, 2], op=ALU.add)
+                hit_of[s, f] = hit
+            hits01 = once.tile([P, BLOCK, PACK], BF16)
+            nc.vector.tensor_tensor(
+                out=hits01[:], in0=hit_of[s, 0][:], in1=hit_of[s, 1][:], op=ALU.add
+            )
+            tied = twice.tile([P, BLOCK, PACK], BF16)
+            nc.vector.tensor_tensor(out=tied[:], in0=hits01[:], in1=hit_of[s, 2][:], op=ALU.add)
+            tie_square = twice.tile([P, BLOCK, PACK], BF16)
+            nc.scalar.activation(
+                out=tie_square[:], in_=tied[:], func=ACT.Square, bias=TIE_SHIFT, scale=TIE_SLOPE
+            )
+            top_of[s] = top
+            tie_square_of[s] = tie_square
 
-                tie_square = twice.tile([P, PACK, BLOCK], BF16)
-                nc.scalar.activation(
-                    out=tie_square[:], in_=tied[:], func=ACT.Square, bias=TIE_SHIFT, scale=TIE_SLOPE
+        def shares(s):
+            w, c0 = s // BLOCKS, (s % BLOCKS) * BLOCK
+            grad_share = once.tile([P, BLOCK, PACK], F32)
+            nc.vector.scalar_tensor_tensor(
+                out=grad_share[:],
+                in0=tie_square_of[s][:],
+                scalar=TIE_OFFSET,
+                in1=grad_words[:, w, c0 : c0 + BLOCK, :],
+                op0=ALU.add,
+                op1=ALU.mult,
+            )
+            neg_grad_top = once.tile([P, BLOCK, PACK], F32)
+            nc.vector.scalar_tensor_tensor(
+                out=neg_grad_top[:],
+                in0=grad_share[:],
+                scalar=-SHARE_SCALE,
+                in1=top_of[s][:],
+                op0=ALU.mult,
+                op1=ALU.mult,
+            )
+            return grad_share, neg_grad_top
+
+        def branch_gradient(s, f, grad_share, neg_grad_top):
+            sg = sg_of[s, f]
+            dpre = branch.tile([P, N_PASS, PACK], BF16, align_bytes=64)
+            nc.vector.scalar_tensor_tensor(
+                out=dpre[:, 0:BLOCK, :],
+                in0=sg[:],
+                scalar=SHARE_SCALE,
+                in1=grad_share[:],
+                op0=ALU.mult,
+                op1=ALU.mult,
+            )
+            nc.vector.scalar_tensor_tensor(
+                out=dpre[:, BLOCK:N_PASS, :],
+                in0=sg[:],
+                scalar=1.0,
+                in1=neg_grad_top[:],
+                op0=ALU.subtract,
+                op1=ALU.mult,
+            )
+            halves = dpre[:].rearrange("p (h c) j -> p h (c j)", h=2)
+            nc.vector.tensor_tensor(
+                out=halves,
+                in0=halves,
+                in1=flat(hit_of[s, f][:]).unsqueeze(1).to_broadcast([P, 2, BLOCK * PACK]),
+                op=ALU.mult,
+            )
+            dpre_of[s, f] = dpre
+
+        def multiply_and_store(s, f):
+            w, c0 = s // BLOCKS, (s % BLOCKS) * BLOCK
+            codes = branch.tile([P, N_PASS], U32, align_bytes=64)
+            scales = branch.tile([P, N_PASS], U8, align_bytes=64)
+            nc.vector.quantize_mx(
+                out=codes[:].bitcast(E5M2_X4), scales=scales[:], in_=flat(dpre_of[s, f][:])
+            )
+            for m in range(M_TILES):
+                m_cols = slice(m * M_TILE, (m + 1) * M_TILE)
+                acc = psum.tile([M_TILE, N_PASS], F32)
+                nc.tensor.matmul_mx(
+                    out=acc[:],
+                    lhsT=agg_codes[:, w, m_cols].bitcast(E4M3_X4),
+                    lhsT_scale=agg_scales[:, w, m_cols],
+                    rhs=codes[:].bitcast(E5M2_X4),
+                    rhs_scale=scales[:],
+                    start=True,
+                    stop=True,
                 )
-                grad_share = once.tile([P, PACK, BLOCK], F32)
-                nc.vector.scalar_tensor_tensor(
-                    out=grad_share[:],
-                    in0=tie_square[:],
-                    scalar=TIE_OFFSET,
-                    in1=grad_rows[:, w, :, c0 : c0 + BLOCK],
-                    op0=ALU.add,
-                    op1=ALU.mult,
-                )
-                neg_grad_top = once.tile([P, PACK, BLOCK], F32)
-                nc.vector.scalar_tensor_tensor(
-                    out=neg_grad_top[:],
-                    in0=grad_share[:],
-                    scalar=-SHARE_SCALE,
-                    in1=top[:],
-                    op0=ALU.mult,
-                    op1=ALU.mult,
+                result = stage.tile([M_TILE, N_PASS], F32)
+                nc.scalar.copy(out=result[:], in_=acc[:])
+                nc.sync.dma_start(
+                    out=out[w, f, m_cols, :].rearrange("p (h c) -> p h c", h=2)[
+                        :, :, c0 : c0 + BLOCK
+                    ],
+                    in_=result[:].rearrange("p (h c) -> p h c", h=2),
                 )
 
-                for f in range(BRANCHES):
-                    dpre = branch.tile([P, PACK, N_PASS], BF16)
-                    nc.vector.scalar_tensor_tensor(
-                        out=dpre[:, :, 0:BLOCK],
-                        in0=sg[:, f],
-                        scalar=SHARE_SCALE,
-                        in1=grad_share[:],
-                        op0=ALU.mult,
-                        op1=ALU.mult,
-                    )
-                    nc.vector.scalar_tensor_tensor(
-                        out=dpre[:, :, BLOCK:N_PASS],
-                        in0=sg[:, f],
-                        scalar=1.0,
-                        in1=neg_grad_top[:],
-                        op0=ALU.subtract,
-                        op1=ALU.mult,
-                    )
-                    halves = dpre[:].rearrange("p j (h c) -> p j h c", h=2)
-                    nc.vector.tensor_tensor(
-                        out=halves,
-                        in0=halves,
-                        in1=hit[:, f].unsqueeze(2).to_broadcast([P, PACK, 2, BLOCK]),
-                        op=ALU.mult,
-                    )
-
-                    grouped = branch.tile([P, N_PASS, PACK], BF16, align_bytes=64)
-                    rows_to_words(nc.scalar.copy, grouped[:], dpre[:])
-                    codes = branch.tile([P, N_PASS], U32, align_bytes=64)
-                    scales = branch.tile([P, N_PASS], U8, align_bytes=64)
-                    nc.vector.quantize_mx(
-                        out=codes[:].bitcast(E5M2_X4),
-                        scales=scales[:],
-                        in_=grouped[:].rearrange("p n j -> p (n j)"),
-                    )
-
-                    for m in range(M_TILES):
-                        m_cols = slice(m * M_TILE, (m + 1) * M_TILE)
-                        acc = psum.tile([M_TILE, N_PASS], F32)
-                        nc.tensor.matmul_mx(
-                            out=acc[:],
-                            lhsT=agg_codes[:, w, m_cols].bitcast(E4M3_X4),
-                            lhsT_scale=agg_scales[:, w, m_cols],
-                            rhs=codes[:].bitcast(E5M2_X4),
-                            rhs_scale=scales[:],
-                            start=True,
-                            stop=True,
-                        )
-                        result = stage.tile([M_TILE, N_PASS], F32)
-                        nc.scalar.copy(out=result[:], in_=acc[:])
-                        nc.sync.dma_start(
-                            out=out[w, f, m_cols, :].rearrange("p (h c) -> p h c", h=2)[
-                                :, :, c0 : c0 + BLOCK
-                            ],
-                            in_=result[:].rearrange("p (h c) -> p h c", h=2),
-                        )
+        for f in range(BRANCHES):
+            load(0, f)
+        load_window(0)
+        for s in range(2):
+            for f in range(BRANCHES):
+                convert(s, f)
+                load(s + 1, f)
+            if s == 0:
+                prepare_window(0)
+                load_window(1)
+        gate_products(0)
+        winners(0)
+        for s in range(SLABS):
+            if s + 1 < SLABS:
+                gate_products(s + 1)
+            grad_share, neg_grad_top = shares(s)
+            for f in range(BRANCHES):
+                branch_gradient(s, f, grad_share, neg_grad_top)
+                if s + 2 < SLABS:
+                    convert(s + 2, f)
+                if s + 3 < SLABS:
+                    load(s + 3, f)
+                if f > 0:
+                    multiply_and_store(s, f - 1)
+            if s == 0:
+                prepare_window(1)
+            if s + 1 < SLABS:
+                winners(s + 1)
+            multiply_and_store(s, BRANCHES - 1)

@@ -55,9 +55,10 @@ def tile_stsindividuallayer_pb_v_kernel(tc, agg, W, b, pre, grad_out, out):
         flags = ctx.enter_context(tc.tile_pool(name="flags", bufs=2 * BRANCHES))
         once = ctx.enter_context(tc.tile_pool(name="once", bufs=1))
         twice = ctx.enter_context(tc.tile_pool(name="twice", bufs=2))
-        branch = ctx.enter_context(tc.tile_pool(name="branch", bufs=3))
+        branch = ctx.enter_context(tc.tile_pool(name="branch", bufs=BRANCHES))
         stage = ctx.enter_context(tc.tile_pool(name="stage", bufs=8))
         psum = ctx.enter_context(tc.psum_pool(name="psum", bufs=8))
+        ctx.enter_context(tc.manual_schedule())
 
         agg_rows = keep.tile([P, WINDOWS, PACK, CHANNELS], BF16)
         grad_rows = keep.tile([P, WINDOWS, PACK, CHANNELS], BF16)
@@ -70,30 +71,30 @@ def tile_stsindividuallayer_pb_v_kernel(tc, agg, W, b, pre, grad_out, out):
         sg_of = {}
         glu_of = {}
         hit_of = {}
+        top01_of = {}
         top_of = {}
+        hits01_of = {}
         tie_square_of = {}
+        grad_share_of = {}
+        neg_grad_top_of = {}
         dpre_of = {}
+        codes_of = {}
+        scales_of = {}
+        agg_words_of = {}
 
-        def load_window(w):
-            nc.sync.dma_start(
-                out=grad_rows[:, w], in_=grad_out[0, w].rearrange("(p j) c -> p j c", j=PACK)
-            )
-            nc.sync.dma_start(
-                out=agg_rows[:, w], in_=agg[0, w].rearrange("(p j) c -> p j c", j=PACK)
-            )
+        def live(s):
+            return 0 <= s < SLABS
 
-        def prepare_window(w):
-            nc.scalar.copy(out=words_in_runs(grad_words[:, w]), in_=rows_in_runs(grad_rows[:, w]))
-            agg_words = once.tile([P, CHANNELS, PACK], BF16, align_bytes=64)
-            nc.scalar.copy(out=words_in_runs(agg_words[:]), in_=rows_in_runs(agg_rows[:, w]))
-            nc.vector.quantize_mx(
-                out=agg_codes[:, w].bitcast(E4M3_X4),
-                scales=agg_scales[:, w],
-                in_=flat(agg_words[:]),
-            )
+        def window(s):
+            return s // BLOCKS
+
+        def first_channel(s):
+            return (s % BLOCKS) * BLOCK
 
         def load(s, f):
-            w, c0 = s // BLOCKS, (s % BLOCKS) * BLOCK
+            if not live(s):
+                return
+            w, c0 = window(s), first_channel(s)
             pre_rows = pre[0, w, f].rearrange("(p j) n -> p j n", j=PACK)
             rhs_rows = raw.tile([P, PACK, BLOCK], F32)
             nc.sync.dma_start(
@@ -103,8 +104,18 @@ def tile_stsindividuallayer_pb_v_kernel(tc, agg, W, b, pre, grad_out, out):
             nc.sync.dma_start(out=lhs_rows[:], in_=pre_rows[:, :, c0 : c0 + BLOCK])
             rhs_rows_of[s, f] = rhs_rows
             lhs_rows_of[s, f] = lhs_rows
+            if f == BRANCHES - 1 and s % BLOCKS == 0:
+                nc.sync.dma_start(
+                    out=grad_rows[:, w], in_=grad_out[0, w].rearrange("(p j) c -> p j c", j=PACK)
+                )
+            if f == BRANCHES - 1 and s % BLOCKS == BLOCKS - 1:
+                nc.sync.dma_start(
+                    out=agg_rows[:, w], in_=agg[0, w].rearrange("(p j) c -> p j c", j=PACK)
+                )
 
         def convert(s, f):
+            if not live(s):
+                return
             sg = words.tile([P, BLOCK, PACK], F32)
             nc.scalar.activation(
                 out=words_in_runs(sg[:]), in_=rows_in_runs(rhs_rows_of[s, f][:]), func=ACT.Sigmoid
@@ -114,94 +125,166 @@ def tile_stsindividuallayer_pb_v_kernel(tc, agg, W, b, pre, grad_out, out):
             sg_of[s, f] = sg
             glu_of[s, f] = glu
 
-        def gate_products(s):
-            for f in range(BRANCHES):
-                glu = glu_of[s, f]
-                nc.vector.tensor_tensor(out=glu[:], in0=glu[:], in1=sg_of[s, f][:], op=ALU.mult)
+        def reorder_grad(s):
+            if live(s) and s % BLOCKS == 0:
+                w = window(s)
+                nc.scalar.copy(
+                    out=words_in_runs(grad_words[:, w]), in_=rows_in_runs(grad_rows[:, w])
+                )
 
-        def winners(s):
+        def reorder_agg(s):
+            if live(s) and s % BLOCKS == 0:
+                agg_words = once.tile([P, CHANNELS, PACK], BF16, align_bytes=64)
+                nc.scalar.copy(
+                    out=words_in_runs(agg_words[:]), in_=rows_in_runs(agg_rows[:, window(s)])
+                )
+                agg_words_of[s] = agg_words
+
+        def quantise_agg(s):
+            if live(s) and s % BLOCKS == 0:
+                w = window(s)
+                nc.vector.quantize_mx(
+                    out=agg_codes[:, w].bitcast(E4M3_X4),
+                    scales=agg_scales[:, w],
+                    in_=flat(agg_words_of[s][:]),
+                )
+
+        def gate_product(s, f):
+            if not live(s):
+                return
+            glu = glu_of[s, f]
+            nc.vector.tensor_tensor(out=glu[:], in0=glu[:], in1=sg_of[s, f][:], op=ALU.mult)
+
+        def first_max(s):
+            if not live(s):
+                return
             top01 = once.tile([P, BLOCK, PACK], F32)
             nc.vector.tensor_tensor(
                 out=top01[:], in0=glu_of[s, 0][:], in1=glu_of[s, 1][:], op=ALU.max
             )
+            top01_of[s] = top01
+
+        def second_max(s):
+            if not live(s):
+                return
             top = twice.tile([P, BLOCK, PACK], F32)
-            nc.vector.tensor_tensor(out=top[:], in0=top01[:], in1=glu_of[s, 2][:], op=ALU.max)
-            for f in range(BRANCHES):
-                hit = flags.tile([P, BLOCK, PACK], BF16)
-                nc.vector.tensor_tensor(
-                    out=hit[:], in0=glu_of[s, f][:], in1=top[:], op=ALU.is_equal
-                )
-                hit_of[s, f] = hit
+            nc.vector.tensor_tensor(
+                out=top[:], in0=top01_of[s][:], in1=glu_of[s, 2][:], op=ALU.max
+            )
+            top_of[s] = top
+
+        def find_hit(s, f):
+            if not live(s):
+                return
+            hit = flags.tile([P, BLOCK, PACK], BF16)
+            nc.vector.tensor_tensor(
+                out=hit[:], in0=glu_of[s, f][:], in1=top_of[s][:], op=ALU.is_equal
+            )
+            hit_of[s, f] = hit
+
+        def count_first_two(s):
+            if not live(s):
+                return
             hits01 = once.tile([P, BLOCK, PACK], BF16)
             nc.vector.tensor_tensor(
                 out=hits01[:], in0=hit_of[s, 0][:], in1=hit_of[s, 1][:], op=ALU.add
             )
+            hits01_of[s] = hits01
+
+        def count_all(s):
+            if not live(s):
+                return
             tied = twice.tile([P, BLOCK, PACK], BF16)
-            nc.vector.tensor_tensor(out=tied[:], in0=hits01[:], in1=hit_of[s, 2][:], op=ALU.add)
+            nc.vector.tensor_tensor(
+                out=tied[:], in0=hits01_of[s][:], in1=hit_of[s, 2][:], op=ALU.add
+            )
             tie_square = twice.tile([P, BLOCK, PACK], BF16)
             nc.scalar.activation(
                 out=tie_square[:], in_=tied[:], func=ACT.Square, bias=TIE_SHIFT, scale=TIE_SLOPE
             )
-            top_of[s] = top
             tie_square_of[s] = tie_square
 
-        def shares(s):
-            w, c0 = s // BLOCKS, (s % BLOCKS) * BLOCK
+        def share_grad(s):
+            if not live(s):
+                return
+            c0 = first_channel(s)
             grad_share = once.tile([P, BLOCK, PACK], F32)
             nc.vector.scalar_tensor_tensor(
                 out=grad_share[:],
                 in0=tie_square_of[s][:],
                 scalar=TIE_OFFSET,
-                in1=grad_words[:, w, c0 : c0 + BLOCK, :],
+                in1=grad_words[:, window(s), c0 : c0 + BLOCK, :],
                 op0=ALU.add,
                 op1=ALU.mult,
             )
+            grad_share_of[s] = grad_share
+
+        def share_grad_times_top(s):
+            if not live(s):
+                return
             neg_grad_top = once.tile([P, BLOCK, PACK], F32)
             nc.vector.scalar_tensor_tensor(
                 out=neg_grad_top[:],
-                in0=grad_share[:],
+                in0=grad_share_of[s][:],
                 scalar=-SHARE_SCALE,
                 in1=top_of[s][:],
                 op0=ALU.mult,
                 op1=ALU.mult,
             )
-            return grad_share, neg_grad_top
+            neg_grad_top_of[s] = neg_grad_top
 
-        def branch_gradient(s, f, grad_share, neg_grad_top):
-            sg = sg_of[s, f]
+        def first_half(s, f):
+            if not live(s):
+                return
             dpre = branch.tile([P, N_PASS, PACK], BF16, align_bytes=64)
             nc.vector.scalar_tensor_tensor(
                 out=dpre[:, 0:BLOCK, :],
-                in0=sg[:],
+                in0=sg_of[s, f][:],
                 scalar=SHARE_SCALE,
-                in1=grad_share[:],
+                in1=grad_share_of[s][:],
                 op0=ALU.mult,
                 op1=ALU.mult,
             )
+            dpre_of[s, f] = dpre
+
+        def second_half(s, f):
+            if not live(s):
+                return
             nc.vector.scalar_tensor_tensor(
-                out=dpre[:, BLOCK:N_PASS, :],
-                in0=sg[:],
+                out=dpre_of[s, f][:, BLOCK:N_PASS, :],
+                in0=sg_of[s, f][:],
                 scalar=1.0,
-                in1=neg_grad_top[:],
+                in1=neg_grad_top_of[s][:],
                 op0=ALU.subtract,
                 op1=ALU.mult,
             )
-            halves = dpre[:].rearrange("p (h c) j -> p h (c j)", h=2)
+
+        def zero_losers(s, f):
+            if not live(s):
+                return
+            halves = dpre_of[s, f][:].rearrange("p (h c) j -> p h (c j)", h=2)
             nc.vector.tensor_tensor(
                 out=halves,
                 in0=halves,
                 in1=flat(hit_of[s, f][:]).unsqueeze(1).to_broadcast([P, 2, BLOCK * PACK]),
                 op=ALU.mult,
             )
-            dpre_of[s, f] = dpre
 
-        def multiply_and_store(s, f):
-            w, c0 = s // BLOCKS, (s % BLOCKS) * BLOCK
+        def quantise(s, f):
+            if not live(s):
+                return
             codes = branch.tile([P, N_PASS], U32, align_bytes=64)
             scales = branch.tile([P, N_PASS], U8, align_bytes=64)
             nc.vector.quantize_mx(
                 out=codes[:].bitcast(E5M2_X4), scales=scales[:], in_=flat(dpre_of[s, f][:])
             )
+            codes_of[s, f] = codes
+            scales_of[s, f] = scales
+
+        def multiply_and_store(s, f):
+            if not live(s):
+                return
+            w, c0 = window(s), first_channel(s)
             for m in range(M_TILES):
                 m_cols = slice(m * M_TILE, (m + 1) * M_TILE)
                 acc = psum.tile([M_TILE, N_PASS], F32)
@@ -209,8 +292,8 @@ def tile_stsindividuallayer_pb_v_kernel(tc, agg, W, b, pre, grad_out, out):
                     out=acc[:],
                     lhsT=agg_codes[:, w, m_cols].bitcast(E4M3_X4),
                     lhsT_scale=agg_scales[:, w, m_cols],
-                    rhs=codes[:].bitcast(E5M2_X4),
-                    rhs_scale=scales[:],
+                    rhs=codes_of[s, f][:].bitcast(E5M2_X4),
+                    rhs_scale=scales_of[s, f][:],
                     start=True,
                     stop=True,
                 )
@@ -225,30 +308,39 @@ def tile_stsindividuallayer_pb_v_kernel(tc, agg, W, b, pre, grad_out, out):
 
         for f in range(BRANCHES):
             load(0, f)
-        load_window(0)
-        for s in range(2):
+        for s in range(-2, SLABS):
+            nxt = s + 1
+            reorder_grad(nxt)
+            reorder_agg(s)
             for f in range(BRANCHES):
-                convert(s, f)
-                load(s + 1, f)
-            if s == 0:
-                prepare_window(0)
-                load_window(1)
-        gate_products(0)
-        winners(0)
-        for s in range(SLABS):
-            if s + 1 < SLABS:
-                gate_products(s + 1)
-            grad_share, neg_grad_top = shares(s)
-            for f in range(BRANCHES):
-                branch_gradient(s, f, grad_share, neg_grad_top)
-                if s + 2 < SLABS:
-                    convert(s + 2, f)
-                if s + 3 < SLABS:
-                    load(s + 3, f)
-                if f > 0:
-                    multiply_and_store(s, f - 1)
-            if s == 0:
-                prepare_window(1)
-            if s + 1 < SLABS:
-                winners(s + 1)
-            multiply_and_store(s, BRANCHES - 1)
+                convert(s + 2, f)
+                load(s + 3, f)
+
+            gate_product(nxt, 0)
+            gate_product(nxt, 1)
+            share_grad(s)
+            gate_product(nxt, 2)
+            share_grad_times_top(s)
+            first_half(s, 0)
+            second_half(s, 0)
+            first_max(nxt)
+            first_half(s, 1)
+            zero_losers(s, 0)
+            second_half(s, 1)
+            quantise_agg(s)
+            quantise(s, 0)
+            multiply_and_store(s, 0)
+            second_max(nxt)
+            first_half(s, 2)
+            zero_losers(s, 1)
+            second_half(s, 2)
+            quantise(s, 1)
+            multiply_and_store(s, 1)
+            find_hit(nxt, 0)
+            find_hit(nxt, 1)
+            zero_losers(s, 2)
+            find_hit(nxt, 2)
+            count_first_two(nxt)
+            quantise(s, 2)
+            count_all(nxt)
+            multiply_and_store(s, 2)

@@ -312,18 +312,18 @@ def tile_stsindividuallayer_pb_v_kernel(tc, agg, W, b, pre, grad_out, out):
             nxt = s + 1
             reorder_grad(nxt)
             reorder_agg(s)
-            for f in range(BRANCHES):
+            for f in range(BRANCHES - 1):
                 convert(s + 2, f)
                 load(s + 3, f)
 
             gate_product(nxt, 0)
             gate_product(nxt, 1)
             share_grad(s)
-            gate_product(nxt, 2)
+            first_max(nxt)
             share_grad_times_top(s)
             first_half(s, 0)
             second_half(s, 0)
-            first_max(nxt)
+            gate_product(nxt, 2)
             first_half(s, 1)
             zero_losers(s, 0)
             second_half(s, 1)
@@ -344,3 +344,6 @@ def tile_stsindividuallayer_pb_v_kernel(tc, agg, W, b, pre, grad_out, out):
             quantise(s, 2)
             count_all(nxt)
             multiply_and_store(s, 2)
+
+            convert(s + 2, BRANCHES - 1)
+            load(s + 3, BRANCHES - 1)

@@ -51,7 +51,9 @@ def tile_stsindividuallayer_pb_v_kernel(tc, agg, W, b, pre, grad_out, out):
     with ExitStack() as ctx:
         keep = ctx.enter_context(tc.tile_pool(name="keep", bufs=1))
         raw = ctx.enter_context(tc.tile_pool(name="raw", bufs=BRANCHES))
+        raw_lhs = ctx.enter_context(tc.tile_pool(name="raw_lhs", bufs=3 * BRANCHES))
         words = ctx.enter_context(tc.tile_pool(name="words", bufs=3 * BRANCHES))
+        products = ctx.enter_context(tc.tile_pool(name="products", bufs=2 * BRANCHES))
         flags = ctx.enter_context(tc.tile_pool(name="flags", bufs=2 * BRANCHES))
         once = ctx.enter_context(tc.tile_pool(name="once", bufs=1))
         twice = ctx.enter_context(tc.tile_pool(name="twice", bufs=2))
@@ -100,7 +102,7 @@ def tile_stsindividuallayer_pb_v_kernel(tc, agg, W, b, pre, grad_out, out):
             nc.sync.dma_start(
                 out=rhs_rows[:], in_=pre_rows[:, :, CHANNELS + c0 : CHANNELS + c0 + BLOCK]
             )
-            lhs_rows = raw.tile([P, PACK, BLOCK], F32)
+            lhs_rows = raw_lhs.tile([P, PACK, BLOCK], F32)
             nc.sync.dma_start(out=lhs_rows[:], in_=pre_rows[:, :, c0 : c0 + BLOCK])
             rhs_rows_of[s, f] = rhs_rows
             lhs_rows_of[s, f] = lhs_rows
@@ -120,10 +122,7 @@ def tile_stsindividuallayer_pb_v_kernel(tc, agg, W, b, pre, grad_out, out):
             nc.scalar.activation(
                 out=words_in_runs(sg[:]), in_=rows_in_runs(rhs_rows_of[s, f][:]), func=ACT.Sigmoid
             )
-            glu = words.tile([P, BLOCK, PACK], F32)
-            nc.scalar.copy(out=words_in_runs(glu[:]), in_=rows_in_runs(lhs_rows_of[s, f][:]))
             sg_of[s, f] = sg
-            glu_of[s, f] = glu
 
         def reorder_grad(s):
             if live(s) and s % BLOCKS == 0:
@@ -152,8 +151,14 @@ def tile_stsindividuallayer_pb_v_kernel(tc, agg, W, b, pre, grad_out, out):
         def gate_product(s, f):
             if not live(s):
                 return
-            glu = glu_of[s, f]
-            nc.vector.tensor_tensor(out=glu[:], in0=glu[:], in1=sg_of[s, f][:], op=ALU.mult)
+            glu = products.tile([P, BLOCK, PACK], F32)
+            nc.vector.tensor_tensor(
+                out=glu[:],
+                in0=lhs_rows_of[s, f][:].rearrange("p j c -> p c j"),
+                in1=sg_of[s, f][:],
+                op=ALU.mult,
+            )
+            glu_of[s, f] = glu
 
         def first_max(s):
             if not live(s):

@@ -1,6 +1,7 @@
 from contextlib import ExitStack
 
 import concourse.mybir as mybir
+from concourse.masks import make_identity
 
 F32 = mybir.dt.float32
 BF16 = mybir.dt.bfloat16
@@ -24,6 +25,12 @@ N_PASS = 2 * BLOCK
 M_TILE = 128
 M_TILES = CHANNELS // M_TILE
 RUN = 4
+SLAB_COLS = BLOCK * PACK
+BANK = 512
+BANKS_A_SLAB = SLAB_COLS // BANK
+TURNS_A_BANK = BANK // P
+TURNS_A_SLAB = SLAB_COLS // P
+GAP_SCALE = 2.0 ** 100
 
 FLOPS = 2 * WINDOWS * BRANCHES * NODES * CHANNELS * 2 * CHANNELS
 BYTES = WINDOWS * NODES * CHANNELS * (2 + 2) + 2 * WINDOWS * BRANCHES * NODES * 2 * CHANNELS * 4
@@ -53,13 +60,17 @@ def tile_stsindividuallayer_pb_v_kernel(tc, agg, W, b, pre, grad_out, out):
         raw = ctx.enter_context(tc.tile_pool(name="raw", bufs=BRANCHES))
         raw_lhs = ctx.enter_context(tc.tile_pool(name="raw_lhs", bufs=3 * BRANCHES))
         words = ctx.enter_context(tc.tile_pool(name="words", bufs=3 * BRANCHES))
-        products = ctx.enter_context(tc.tile_pool(name="products", bufs=2 * BRANCHES))
-        flags = ctx.enter_context(tc.tile_pool(name="flags", bufs=2 * BRANCHES))
+        products = ctx.enter_context(tc.tile_pool(name="products", bufs=BRANCHES))
+        flags = ctx.enter_context(tc.tile_pool(name="flags", bufs=BRANCHES))
         once = ctx.enter_context(tc.tile_pool(name="once", bufs=1))
         twice = ctx.enter_context(tc.tile_pool(name="twice", bufs=2))
         branch = ctx.enter_context(tc.tile_pool(name="branch", bufs=BRANCHES))
+        turned = ctx.enter_context(tc.tile_pool(name="turned", bufs=BRANCHES))
         stage = ctx.enter_context(tc.tile_pool(name="stage", bufs=8))
-        psum = ctx.enter_context(tc.psum_pool(name="psum", bufs=8))
+        psum = ctx.enter_context(tc.psum_pool(name="psum", bufs=2))
+        psum_gap = ctx.enter_context(tc.psum_pool(name="psum_gap", bufs=2))
+        psum_hit = ctx.enter_context(tc.psum_pool(name="psum_hit", bufs=BRANCHES))
+        psum_count = ctx.enter_context(tc.psum_pool(name="psum_count", bufs=1))
         ctx.enter_context(tc.manual_schedule())
 
         agg_rows = keep.tile([P, WINDOWS, PACK, CHANNELS], BF16)
@@ -68,6 +79,13 @@ def tile_stsindividuallayer_pb_v_kernel(tc, agg, W, b, pre, grad_out, out):
         agg_codes = keep.tile([P, WINDOWS, CHANNELS], U32, align_bytes=64)
         agg_scales = keep.tile([P, WINDOWS, CHANNELS], U8, align_bytes=64)
 
+        ident_f32 = keep.tile([P, P], F32)
+        make_identity(nc, ident_f32[:])
+        ident_bf16 = keep.tile([P, P], BF16)
+        make_identity(nc, ident_bf16[:])
+
+        neg_top_of = {}
+        hit_t_of = {}
         rhs_rows_of = {}
         lhs_rows_of = {}
         sg_of = {}
@@ -185,14 +203,14 @@ def tile_stsindividuallayer_pb_v_kernel(tc, agg, W, b, pre, grad_out, out):
             nc.vector.tensor_tensor(
                 out=hit[:], in0=glu_of[s, f][:], in1=top_of[s][:], op=ALU.is_equal
             )
-            hit_of[s, f] = hit
+            hit_of[s, f] = flat(hit[:])
 
         def count_first_two(s):
             if not live(s):
                 return
             hits01 = once.tile([P, BLOCK, PACK], BF16)
             nc.vector.tensor_tensor(
-                out=hits01[:], in0=hit_of[s, 0][:], in1=hit_of[s, 1][:], op=ALU.add
+                out=flat(hits01[:]), in0=hit_of[s, 0], in1=hit_of[s, 1], op=ALU.add
             )
             hits01_of[s] = hits01
 
@@ -201,13 +219,94 @@ def tile_stsindividuallayer_pb_v_kernel(tc, agg, W, b, pre, grad_out, out):
                 return
             tied = twice.tile([P, BLOCK, PACK], BF16)
             nc.vector.tensor_tensor(
-                out=tied[:], in0=hits01_of[s][:], in1=hit_of[s, 2][:], op=ALU.add
+                out=flat(tied[:]), in0=flat(hits01_of[s][:]), in1=hit_of[s, 2], op=ALU.add
             )
-            tie_square = twice.tile([P, BLOCK, PACK], BF16)
+            tie_square = twice.tile([P, SLAB_COLS], BF16)
             nc.scalar.activation(
-                out=tie_square[:], in_=tied[:], func=ACT.Square, bias=TIE_SHIFT, scale=TIE_SLOPE
+                out=tie_square[:],
+                in_=flat(tied[:]),
+                func=ACT.Square,
+                bias=TIE_SHIFT,
+                scale=TIE_SLOPE,
             )
             tie_square_of[s] = tie_square
+
+        def negate_top(s):
+            if not live(s):
+                return
+            neg_top = twice.tile([P, SLAB_COLS], F32)
+            nc.scalar.activation(
+                out=neg_top[:], in_=flat(top_of[s][:]), func=ACT.Copy, scale=-1.0
+            )
+            neg_top_of[s] = neg_top
+
+        def find_hit_turned(s, f, bank):
+            if not live(s):
+                return
+            if bank == 0:
+                hit_t = turned.tile([P, SLAB_COLS], BF16)
+                hit_t_of[s, f] = hit_t
+            gap_t = psum_gap.tile([P, BANK], F32)
+            for turn in range(TURNS_A_BANK):
+                cols = slice(bank * BANK + turn * P, bank * BANK + (turn + 1) * P)
+                here = gap_t[:, turn * P : (turn + 1) * P]
+                nc.tensor.matmul(
+                    out=here,
+                    lhsT=flat(glu_of[s, f][:])[:, cols],
+                    rhs=ident_f32[:],
+                    is_transpose=True,
+                    start=True,
+                    stop=False,
+                )
+                nc.tensor.matmul(
+                    out=here,
+                    lhsT=neg_top_of[s][:, cols],
+                    rhs=ident_f32[:],
+                    is_transpose=True,
+                    start=False,
+                    stop=True,
+                )
+            nc.scalar.activation(
+                out=hit_t_of[s, f][:, bank * BANK : (bank + 1) * BANK],
+                in_=gap_t[:],
+                func=ACT.Relu,
+                bias=1.0,
+                scale=GAP_SCALE,
+            )
+
+        def count_turning_back(s, bank):
+            if not live(s):
+                return
+            if bank == 0:
+                tie_square = twice.tile([P, SLAB_COLS], BF16)
+                tie_square_of[s] = tie_square
+            count = psum_count.tile([P, BANK], F32)
+            for turn in range(TURNS_A_BANK):
+                cols = slice(bank * BANK + turn * P, bank * BANK + (turn + 1) * P)
+                for f in range(BRANCHES):
+                    nc.tensor.matmul(
+                        out=count[:, turn * P : (turn + 1) * P],
+                        lhsT=hit_t_of[s, f][:, cols],
+                        rhs=ident_bf16[:],
+                        start=(f == 0),
+                        stop=(f == BRANCHES - 1),
+                    )
+            nc.scalar.activation(
+                out=tie_square_of[s][:, bank * BANK : (bank + 1) * BANK],
+                in_=count[:],
+                func=ACT.Square,
+                bias=TIE_SHIFT,
+                scale=TIE_SLOPE,
+            )
+
+        def turn_hit_back(s, f):
+            if not live(s):
+                return
+            hit_back = psum_hit.tile([P, SLAB_COLS], BF16)
+            for turn in range(TURNS_A_SLAB):
+                cols = slice(turn * P, (turn + 1) * P)
+                nc.tensor.transpose(hit_back[:, cols], hit_t_of[s, f][:, cols], ident_bf16[:])
+            hit_of[s, f] = hit_back[:]
 
         def share_grad(s):
             if not live(s):
@@ -215,10 +314,10 @@ def tile_stsindividuallayer_pb_v_kernel(tc, agg, W, b, pre, grad_out, out):
             c0 = first_channel(s)
             grad_share = once.tile([P, BLOCK, PACK], F32)
             nc.vector.scalar_tensor_tensor(
-                out=grad_share[:],
+                out=flat(grad_share[:]),
                 in0=tie_square_of[s][:],
                 scalar=TIE_OFFSET,
-                in1=grad_words[:, window(s), c0 : c0 + BLOCK, :],
+                in1=flat(grad_words[:, window(s), c0 : c0 + BLOCK, :]),
                 op0=ALU.add,
                 op1=ALU.mult,
             )
@@ -271,7 +370,7 @@ def tile_stsindividuallayer_pb_v_kernel(tc, agg, W, b, pre, grad_out, out):
             nc.vector.tensor_tensor(
                 out=halves,
                 in0=halves,
-                in1=flat(hit_of[s, f][:]).unsqueeze(1).to_broadcast([P, 2, BLOCK * PACK]),
+                in1=hit_of[s, f].unsqueeze(1).to_broadcast([P, 2, SLAB_COLS]),
                 op=ALU.mult,
             )
 
@@ -313,42 +412,59 @@ def tile_stsindividuallayer_pb_v_kernel(tc, agg, W, b, pre, grad_out, out):
 
         for f in range(BRANCHES):
             load(0, f)
-        for s in range(-2, SLABS):
+        for s in range(-2, SLABS + 1):
             nxt = s + 1
-            reorder_grad(nxt)
-            reorder_agg(s)
-            for f in range(BRANCHES - 1):
-                convert(s + 2, f)
-                load(s + 3, f)
+            ahead = s + 2
+            last = BRANCHES - 1
 
             gate_product(nxt, 0)
+            quantise(s - 1, last)
+            multiply_and_store(s - 1, last)
+            reorder_grad(nxt)
+            reorder_agg(s)
+            convert(ahead, 0)
+            load(ahead + 1, 0)
             gate_product(nxt, 1)
             share_grad(s)
             first_max(nxt)
+            convert(ahead, 1)
+            load(ahead + 1, 1)
+            gate_product(nxt, 2)
             share_grad_times_top(s)
+            convert(ahead, 2)
+            load(ahead + 1, 2)
+            second_max(nxt)
+            if nxt == 0:
+                for f in range(BRANCHES):
+                    find_hit(nxt, f)
+                count_first_two(nxt)
+                count_all(nxt)
+            else:
+                negate_top(nxt)
+                for f in range(BRANCHES):
+                    for bank in range(BANKS_A_SLAB):
+                        find_hit_turned(nxt, f, bank)
+
             first_half(s, 0)
             second_half(s, 0)
-            gate_product(nxt, 2)
             first_half(s, 1)
             zero_losers(s, 0)
             second_half(s, 1)
+            if nxt != 0:
+                turn_hit_back(nxt, 0)
             quantise_agg(s)
             quantise(s, 0)
             multiply_and_store(s, 0)
-            second_max(nxt)
+            if nxt != 0:
+                for bank in range(BANKS_A_SLAB):
+                    count_turning_back(nxt, bank)
             first_half(s, 2)
             zero_losers(s, 1)
+            if nxt != 0:
+                turn_hit_back(nxt, 1)
             second_half(s, 2)
             quantise(s, 1)
             multiply_and_store(s, 1)
-            find_hit(nxt, 0)
-            find_hit(nxt, 1)
-            zero_losers(s, 2)
-            find_hit(nxt, 2)
-            count_first_two(nxt)
-            quantise(s, 2)
-            count_all(nxt)
-            multiply_and_store(s, 2)
-
-            convert(s + 2, BRANCHES - 1)
-            load(s + 3, BRANCHES - 1)
+            zero_losers(s, last)
+            if nxt != 0:
+                turn_hit_back(nxt, last)

@@ -58,19 +58,18 @@ def tile_stsindividuallayer_pb_v_kernel(tc, agg, W, b, pre, grad_out, out):
     with ExitStack() as ctx:
         keep = ctx.enter_context(tc.tile_pool(name="keep", bufs=1))
         raw = ctx.enter_context(tc.tile_pool(name="raw", bufs=BRANCHES))
-        raw_lhs = ctx.enter_context(tc.tile_pool(name="raw_lhs", bufs=3 * BRANCHES))
-        words = ctx.enter_context(tc.tile_pool(name="words", bufs=3 * BRANCHES))
-        products = ctx.enter_context(tc.tile_pool(name="products", bufs=BRANCHES))
+        raw_lhs = ctx.enter_context(tc.tile_pool(name="raw_lhs", bufs=2 * BRANCHES))
+        words = ctx.enter_context(tc.tile_pool(name="words", bufs=4 * BRANCHES))
+        products = ctx.enter_context(tc.tile_pool(name="products", bufs=2 * BRANCHES))
         flags = ctx.enter_context(tc.tile_pool(name="flags", bufs=BRANCHES))
         once = ctx.enter_context(tc.tile_pool(name="once", bufs=1))
-        twice = ctx.enter_context(tc.tile_pool(name="twice", bufs=2))
+        thrice = ctx.enter_context(tc.tile_pool(name="thrice", bufs=3))
         branch = ctx.enter_context(tc.tile_pool(name="branch", bufs=BRANCHES))
-        turned = ctx.enter_context(tc.tile_pool(name="turned", bufs=BRANCHES))
-        stage = ctx.enter_context(tc.tile_pool(name="stage", bufs=8))
+        turned = ctx.enter_context(tc.tile_pool(name="turned", bufs=2 * BRANCHES))
+        stage = ctx.enter_context(tc.tile_pool(name="stage", bufs=4))
         psum = ctx.enter_context(tc.psum_pool(name="psum", bufs=2))
-        psum_gap = ctx.enter_context(tc.psum_pool(name="psum_gap", bufs=2))
+        psum_gap = ctx.enter_context(tc.psum_pool(name="psum_gap", bufs=3))
         psum_hit = ctx.enter_context(tc.psum_pool(name="psum_hit", bufs=BRANCHES))
-        psum_count = ctx.enter_context(tc.psum_pool(name="psum_count", bufs=1))
         ctx.enter_context(tc.manual_schedule())
 
         agg_rows = keep.tile([P, WINDOWS, PACK, CHANNELS], BF16)
@@ -111,18 +110,24 @@ def tile_stsindividuallayer_pb_v_kernel(tc, agg, W, b, pre, grad_out, out):
         def first_channel(s):
             return (s % BLOCKS) * BLOCK
 
-        def load(s, f):
+        def load_rhs(s, f):
             if not live(s):
                 return
-            w, c0 = window(s), first_channel(s)
-            pre_rows = pre[0, w, f].rearrange("(p j) n -> p j n", j=PACK)
+            c0 = first_channel(s)
+            pre_rows = pre[0, window(s), f].rearrange("(p j) n -> p j n", j=PACK)
             rhs_rows = raw.tile([P, PACK, BLOCK], F32)
             nc.sync.dma_start(
                 out=rhs_rows[:], in_=pre_rows[:, :, CHANNELS + c0 : CHANNELS + c0 + BLOCK]
             )
+            rhs_rows_of[s, f] = rhs_rows
+
+        def load_lhs(s, f):
+            if not live(s):
+                return
+            w, c0 = window(s), first_channel(s)
+            pre_rows = pre[0, w, f].rearrange("(p j) n -> p j n", j=PACK)
             lhs_rows = raw_lhs.tile([P, PACK, BLOCK], F32)
             nc.sync.dma_start(out=lhs_rows[:], in_=pre_rows[:, :, c0 : c0 + BLOCK])
-            rhs_rows_of[s, f] = rhs_rows
             lhs_rows_of[s, f] = lhs_rows
             if f == BRANCHES - 1 and s % BLOCKS == 0:
                 nc.sync.dma_start(
@@ -190,7 +195,7 @@ def tile_stsindividuallayer_pb_v_kernel(tc, agg, W, b, pre, grad_out, out):
         def second_max(s):
             if not live(s):
                 return
-            top = twice.tile([P, BLOCK, PACK], F32)
+            top = thrice.tile([P, BLOCK, PACK], F32)
             nc.vector.tensor_tensor(
                 out=top[:], in0=top01_of[s][:], in1=glu_of[s, 2][:], op=ALU.max
             )
@@ -217,11 +222,11 @@ def tile_stsindividuallayer_pb_v_kernel(tc, agg, W, b, pre, grad_out, out):
         def count_all(s):
             if not live(s):
                 return
-            tied = twice.tile([P, BLOCK, PACK], BF16)
+            tied = once.tile([P, BLOCK, PACK], BF16)
             nc.vector.tensor_tensor(
                 out=flat(tied[:]), in0=flat(hits01_of[s][:]), in1=hit_of[s, 2], op=ALU.add
             )
-            tie_square = twice.tile([P, SLAB_COLS], BF16)
+            tie_square = thrice.tile([P, SLAB_COLS], BF16)
             nc.scalar.activation(
                 out=tie_square[:],
                 in_=flat(tied[:]),
@@ -234,7 +239,7 @@ def tile_stsindividuallayer_pb_v_kernel(tc, agg, W, b, pre, grad_out, out):
         def negate_top(s):
             if not live(s):
                 return
-            neg_top = twice.tile([P, SLAB_COLS], F32)
+            neg_top = thrice.tile([P, SLAB_COLS], F32)
             nc.scalar.activation(
                 out=neg_top[:], in_=flat(top_of[s][:]), func=ACT.Copy, scale=-1.0
             )
@@ -246,7 +251,7 @@ def tile_stsindividuallayer_pb_v_kernel(tc, agg, W, b, pre, grad_out, out):
             if bank == 0:
                 hit_t = turned.tile([P, SLAB_COLS], BF16)
                 hit_t_of[s, f] = hit_t
-            gap_t = psum_gap.tile([P, BANK], F32)
+            gap_t = psum_gap.tile([P, BANK], F32, tag="turn")
             for turn in range(TURNS_A_BANK):
                 cols = slice(bank * BANK + turn * P, bank * BANK + (turn + 1) * P)
                 here = gap_t[:, turn * P : (turn + 1) * P]
@@ -278,9 +283,9 @@ def tile_stsindividuallayer_pb_v_kernel(tc, agg, W, b, pre, grad_out, out):
             if not live(s):
                 return
             if bank == 0:
-                tie_square = twice.tile([P, SLAB_COLS], BF16)
+                tie_square = thrice.tile([P, SLAB_COLS], BF16)
                 tie_square_of[s] = tie_square
-            count = psum_count.tile([P, BANK], F32)
+            count = psum_gap.tile([P, BANK], F32, tag="turn")
             for turn in range(TURNS_A_BANK):
                 cols = slice(bank * BANK + turn * P, bank * BANK + (turn + 1) * P)
                 for f in range(BRANCHES):
@@ -328,10 +333,10 @@ def tile_stsindividuallayer_pb_v_kernel(tc, agg, W, b, pre, grad_out, out):
                 return
             neg_grad_top = once.tile([P, BLOCK, PACK], F32)
             nc.vector.scalar_tensor_tensor(
-                out=neg_grad_top[:],
-                in0=grad_share_of[s][:],
-                scalar=-SHARE_SCALE,
-                in1=top_of[s][:],
+                out=flat(neg_grad_top[:]),
+                in0=flat(grad_share_of[s][:]),
+                scalar=SHARE_SCALE,
+                in1=neg_top_of[s][:],
                 op0=ALU.mult,
                 op1=ALU.mult,
             )
@@ -385,11 +390,11 @@ def tile_stsindividuallayer_pb_v_kernel(tc, agg, W, b, pre, grad_out, out):
             codes_of[s, f] = codes
             scales_of[s, f] = scales
 
-        def multiply_and_store(s, f):
+        def multiply_and_store(s, f, m_tiles):
             if not live(s):
                 return
             w, c0 = window(s), first_channel(s)
-            for m in range(M_TILES):
+            for m in m_tiles:
                 m_cols = slice(m * M_TILE, (m + 1) * M_TILE)
                 acc = psum.tile([M_TILE, N_PASS], F32)
                 nc.tensor.matmul_mx(
@@ -410,61 +415,83 @@ def tile_stsindividuallayer_pb_v_kernel(tc, agg, W, b, pre, grad_out, out):
                     in_=result[:].rearrange("p (h c) -> p h c", h=2),
                 )
 
+        last = BRANCHES - 1
+        on_vector = 0
+
+        def turned_path(s):
+            return live(s) and s != on_vector
+
+        def convert_and_load(s, f):
+            convert(s, f)
+            load_rhs(s + 1, f)
+            load_lhs(s + 1, f)
+
+        def hit_turned(s, f, bank):
+            if turned_path(s):
+                find_hit_turned(s, f, bank)
+
+        def count_turned(s, bank):
+            if turned_path(s):
+                count_turning_back(s, bank)
+
+        def hit_back(s, f):
+            if turned_path(s):
+                turn_hit_back(s, f)
+
+        first_rows = range(0, M_TILES // 2)
+        other_rows = range(M_TILES // 2, M_TILES)
         for f in range(BRANCHES):
-            load(0, f)
-        for s in range(-2, SLABS + 1):
+            load_rhs(0, f)
+            load_lhs(0, f)
+        for s in range(-3, SLABS + 1):
             nxt = s + 1
-            ahead = s + 2
-            last = BRANCHES - 1
-
-            gate_product(nxt, 0)
+            far = s + 2
+            gate_product(far, 0)
+            convert_and_load(far + 1, 0)
+            hit_turned(nxt, last, 0)
             quantise(s - 1, last)
-            multiply_and_store(s - 1, last)
-            reorder_grad(nxt)
-            reorder_agg(s)
-            convert(ahead, 0)
-            load(ahead + 1, 0)
-            gate_product(nxt, 1)
+            multiply_and_store(s - 1, last, first_rows)
+            hit_turned(nxt, last, 1)
+            multiply_and_store(s - 1, last, other_rows)
+            count_turned(nxt, 0)
+            gate_product(far, 1)
             share_grad(s)
-            first_max(nxt)
-            convert(ahead, 1)
-            load(ahead + 1, 1)
-            gate_product(nxt, 2)
+            first_max(far)
+            count_turned(nxt, 1)
+            gate_product(far, 2)
             share_grad_times_top(s)
-            convert(ahead, 2)
-            load(ahead + 1, 2)
-            second_max(nxt)
-            if nxt == 0:
-                for f in range(BRANCHES):
-                    find_hit(nxt, f)
-                count_first_two(nxt)
-                count_all(nxt)
-            else:
-                negate_top(nxt)
-                for f in range(BRANCHES):
-                    for bank in range(BANKS_A_SLAB):
-                        find_hit_turned(nxt, f, bank)
-
+            second_max(far)
+            negate_top(far)
+            convert_and_load(far + 1, 1)
+            hit_turned(far, 0, 0)
+            convert_and_load(far + 1, 2)
+            hit_turned(far, 0, 1)
+            if far == on_vector:
+                find_hit(far, 0)
+                find_hit(far, 1)
+                find_hit(far, 2)
+                count_first_two(far)
+                count_all(far)
             first_half(s, 0)
             second_half(s, 0)
             first_half(s, 1)
             zero_losers(s, 0)
             second_half(s, 1)
-            if nxt != 0:
-                turn_hit_back(nxt, 0)
+            hit_back(nxt, 0)
             quantise_agg(s)
             quantise(s, 0)
-            multiply_and_store(s, 0)
-            if nxt != 0:
-                for bank in range(BANKS_A_SLAB):
-                    count_turning_back(nxt, bank)
+            multiply_and_store(s, 0, first_rows)
+            hit_turned(far, 1, 0)
+            multiply_and_store(s, 0, other_rows)
+            reorder_grad(far)
+            reorder_agg(nxt)
             first_half(s, 2)
             zero_losers(s, 1)
-            if nxt != 0:
-                turn_hit_back(nxt, 1)
+            hit_back(nxt, 1)
             second_half(s, 2)
             quantise(s, 1)
-            multiply_and_store(s, 1)
+            multiply_and_store(s, 1, first_rows)
+            hit_turned(far, 1, 1)
+            multiply_and_store(s, 1, other_rows)
             zero_losers(s, last)
-            if nxt != 0:
-                turn_hit_back(nxt, last)
+            hit_back(nxt, last)

@@ -63,10 +63,11 @@ def tile_stsindividuallayer_pb_v_kernel(tc, agg, W, b, pre, grad_out, out):
         products = ctx.enter_context(tc.tile_pool(name="products", bufs=2 * BRANCHES))
         flags = ctx.enter_context(tc.tile_pool(name="flags", bufs=BRANCHES))
         once = ctx.enter_context(tc.tile_pool(name="once", bufs=1))
+        pairs2 = ctx.enter_context(tc.tile_pool(name="pairs2", bufs=2))
         thrice = ctx.enter_context(tc.tile_pool(name="thrice", bufs=3))
         branch = ctx.enter_context(tc.tile_pool(name="branch", bufs=BRANCHES))
         turned = ctx.enter_context(tc.tile_pool(name="turned", bufs=2 * BRANCHES))
-        stage = ctx.enter_context(tc.tile_pool(name="stage", bufs=4))
+        stage = ctx.enter_context(tc.tile_pool(name="stage", bufs=6))
         psum = ctx.enter_context(tc.psum_pool(name="psum", bufs=2))
         psum_gap = ctx.enter_context(tc.psum_pool(name="psum_gap", bufs=3))
         psum_hit = ctx.enter_context(tc.psum_pool(name="psum_hit", bufs=BRANCHES))
@@ -195,7 +196,7 @@ def tile_stsindividuallayer_pb_v_kernel(tc, agg, W, b, pre, grad_out, out):
         def second_max(s):
             if not live(s):
                 return
-            top = thrice.tile([P, BLOCK, PACK], F32)
+            top = pairs2.tile([P, BLOCK, PACK], F32)
             nc.vector.tensor_tensor(
                 out=top[:], in0=top01_of[s][:], in1=glu_of[s, 2][:], op=ALU.max
             )
@@ -396,7 +397,11 @@ def tile_stsindividuallayer_pb_v_kernel(tc, agg, W, b, pre, grad_out, out):
             w, c0 = window(s), first_channel(s)
             for m in m_tiles:
                 m_cols = slice(m * M_TILE, (m + 1) * M_TILE)
-                acc = psum.tile([M_TILE, N_PASS], F32)
+                closing = s == SLABS - 1 and m % 2 == 1
+                if closing:
+                    acc = psum_gap.tile([M_TILE, N_PASS], F32, tag="turn")
+                else:
+                    acc = psum.tile([M_TILE, N_PASS], F32)
                 nc.tensor.matmul_mx(
                     out=acc[:],
                     lhsT=agg_codes[:, w, m_cols].bitcast(E4M3_X4),
@@ -407,7 +412,10 @@ def tile_stsindividuallayer_pb_v_kernel(tc, agg, W, b, pre, grad_out, out):
                     stop=True,
                 )
                 result = stage.tile([M_TILE, N_PASS], F32)
-                nc.scalar.copy(out=result[:], in_=acc[:])
+                if closing and f == BRANCHES - 1:
+                    nc.vector.tensor_copy(out=result[:], in_=acc[:])
+                else:
+                    nc.scalar.copy(out=result[:], in_=acc[:])
                 nc.sync.dma_start(
                     out=out[w, f, m_cols, :].rearrange("p (h c) -> p h c", h=2)[
                         :, :, c0 : c0 + BLOCK
@@ -446,6 +454,8 @@ def tile_stsindividuallayer_pb_v_kernel(tc, agg, W, b, pre, grad_out, out):
         for s in range(-3, SLABS + 1):
             nxt = s + 1
             far = s + 2
+            if nxt == on_vector:
+                find_hit(nxt, 0)
             gate_product(far, 0)
             convert_and_load(far + 1, 0)
             hit_turned(nxt, last, 0)
@@ -454,6 +464,9 @@ def tile_stsindividuallayer_pb_v_kernel(tc, agg, W, b, pre, grad_out, out):
             hit_turned(nxt, last, 1)
             multiply_and_store(s - 1, last, other_rows)
             count_turned(nxt, 0)
+            convert_and_load(far + 1, 1)
+            if nxt == on_vector:
+                find_hit(nxt, 1)
             gate_product(far, 1)
             share_grad(s)
             first_max(far)
@@ -462,16 +475,13 @@ def tile_stsindividuallayer_pb_v_kernel(tc, agg, W, b, pre, grad_out, out):
             share_grad_times_top(s)
             second_max(far)
             negate_top(far)
-            convert_and_load(far + 1, 1)
+            if nxt == on_vector:
+                find_hit(nxt, 2)
+                count_first_two(nxt)
+                count_all(nxt)
             hit_turned(far, 0, 0)
             convert_and_load(far + 1, 2)
             hit_turned(far, 0, 1)
-            if far == on_vector:
-                find_hit(far, 0)
-                find_hit(far, 1)
-                find_hit(far, 2)
-                count_first_two(far)
-                count_all(far)
             first_half(s, 0)
             second_half(s, 0)
             first_half(s, 1)

@@ -457,24 +457,24 @@ def tile_stsindividuallayer_pb_v_kernel(tc, agg, W, b, pre, grad_out, out):
             if nxt == on_vector:
                 find_hit(nxt, 0)
             gate_product(far, 0)
-            convert_and_load(far + 1, 0)
-            hit_turned(nxt, last, 0)
             quantise(s - 1, last)
-            multiply_and_store(s - 1, last, first_rows)
-            hit_turned(nxt, last, 1)
-            multiply_and_store(s - 1, last, other_rows)
-            count_turned(nxt, 0)
-            convert_and_load(far + 1, 1)
             if nxt == on_vector:
                 find_hit(nxt, 1)
             gate_product(far, 1)
             share_grad(s)
             first_max(far)
-            count_turned(nxt, 1)
             gate_product(far, 2)
             share_grad_times_top(s)
             second_max(far)
+            convert_and_load(far + 1, 0)
+            hit_turned(nxt, last, 0)
+            multiply_and_store(s - 1, last, first_rows)
+            hit_turned(nxt, last, 1)
             negate_top(far)
+            multiply_and_store(s - 1, last, other_rows)
+            count_turned(nxt, 0)
+            convert_and_load(far + 1, 1)
+            count_turned(nxt, 1)
             if nxt == on_vector:
                 find_hit(nxt, 2)
                 count_first_two(nxt)

@@ -31,14 +31,15 @@ BANKS_A_SLAB = SLAB_COLS // BANK
 TURNS_A_BANK = BANK // P
 TURNS_A_SLAB = SLAB_COLS // P
 GAP_SCALE = 2.0 ** 100
+FIRST_ON_GPSIMD = 2
 
 FLOPS = 2 * WINDOWS * BRANCHES * NODES * CHANNELS * 2 * CHANNELS
 BYTES = WINDOWS * NODES * CHANNELS * (2 + 2) + 2 * WINDOWS * BRANCHES * NODES * 2 * CHANNELS * 4
 
-TIE_SLOPE = 0.25
-TIE_SHIFT = -0.75
-TIE_OFFSET = 0.125
-SHARE_SCALE = 8.0 / 3.0
+TIE_ROOT = (8.0 / 3.0) ** 0.5
+TIE_SLOPE = 0.25 * TIE_ROOT
+TIE_SHIFT = -0.75 * TIE_ROOT
+TIE_OFFSET = 1.0 / 3.0
 
 
 def rows_in_runs(rows):
@@ -227,7 +228,7 @@ def tile_stsindividuallayer_pb_v_kernel(tc, agg, W, b, pre, grad_out, out):
             nc.vector.tensor_tensor(
                 out=flat(tied[:]), in0=flat(hits01_of[s][:]), in1=hit_of[s, 2], op=ALU.add
             )
-            tie_square = thrice.tile([P, SLAB_COLS], BF16)
+            tie_square = pairs2.tile([P, SLAB_COLS], F32)
             nc.scalar.activation(
                 out=tie_square[:],
                 in_=flat(tied[:]),
@@ -284,7 +285,7 @@ def tile_stsindividuallayer_pb_v_kernel(tc, agg, W, b, pre, grad_out, out):
             if not live(s):
                 return
             if bank == 0:
-                tie_square = thrice.tile([P, SLAB_COLS], BF16)
+                tie_square = pairs2.tile([P, SLAB_COLS], F32)
                 tie_square_of[s] = tie_square
             count = psum_gap.tile([P, BANK], F32, tag="turn")
             for turn in range(TURNS_A_BANK):
@@ -333,13 +334,12 @@ def tile_stsindividuallayer_pb_v_kernel(tc, agg, W, b, pre, grad_out, out):
             if not live(s):
                 return
             neg_grad_top = once.tile([P, BLOCK, PACK], F32)
-            nc.vector.scalar_tensor_tensor(
+            engine = nc.gpsimd if s >= FIRST_ON_GPSIMD else nc.vector
+            engine.tensor_tensor(
                 out=flat(neg_grad_top[:]),
                 in0=flat(grad_share_of[s][:]),
-                scalar=SHARE_SCALE,
                 in1=neg_top_of[s][:],
-                op0=ALU.mult,
-                op1=ALU.mult,
+                op=ALU.mult,
             )
             neg_grad_top_of[s] = neg_grad_top
 
@@ -347,13 +347,8 @@ def tile_stsindividuallayer_pb_v_kernel(tc, agg, W, b, pre, grad_out, out):
             if not live(s):
                 return
             dpre = branch.tile([P, N_PASS, PACK], BF16, align_bytes=64)
-            nc.vector.scalar_tensor_tensor(
-                out=dpre[:, 0:BLOCK, :],
-                in0=sg_of[s, f][:],
-                scalar=SHARE_SCALE,
-                in1=grad_share_of[s][:],
-                op0=ALU.mult,
-                op1=ALU.mult,
+            nc.vector.tensor_tensor(
+                out=dpre[:, 0:BLOCK, :], in0=sg_of[s, f][:], in1=grad_share_of[s][:], op=ALU.mult
             )
             dpre_of[s, f] = dpre
 
@@ -457,24 +452,35 @@ def tile_stsindividuallayer_pb_v_kernel(tc, agg, W, b, pre, grad_out, out):
             if nxt == on_vector:
                 find_hit(nxt, 0)
             gate_product(far, 0)
-            quantise(s - 1, last)
+            share_grad(s)
+            if s >= FIRST_ON_GPSIMD:
+                share_grad_times_top(s)
+            zero_losers(s - 1, 1)
+            hit_back(s, 1)
+            zero_losers(s - 1, last)
+            hit_back(s, last)
+            if s < FIRST_ON_GPSIMD:
+                share_grad_times_top(s)
             if nxt == on_vector:
                 find_hit(nxt, 1)
             gate_product(far, 1)
-            share_grad(s)
+            quantise(s - 1, 1)
             first_max(far)
+            quantise(s - 1, last)
             gate_product(far, 2)
-            share_grad_times_top(s)
+            first_half(s, 0)
             second_max(far)
             convert_and_load(far + 1, 0)
             hit_turned(nxt, last, 0)
-            multiply_and_store(s - 1, last, first_rows)
+            multiply_and_store(s - 1, 1, first_rows)
             hit_turned(nxt, last, 1)
             negate_top(far)
-            multiply_and_store(s - 1, last, other_rows)
+            multiply_and_store(s - 1, 1, other_rows)
             count_turned(nxt, 0)
-            convert_and_load(far + 1, 1)
+            multiply_and_store(s - 1, last, first_rows)
             count_turned(nxt, 1)
+            multiply_and_store(s - 1, last, other_rows)
+            convert_and_load(far + 1, 1)
             if nxt == on_vector:
                 find_hit(nxt, 2)
                 count_first_two(nxt)
@@ -482,12 +488,11 @@ def tile_stsindividuallayer_pb_v_kernel(tc, agg, W, b, pre, grad_out, out):
             hit_turned(far, 0, 0)
             convert_and_load(far + 1, 2)
             hit_turned(far, 0, 1)
-            first_half(s, 0)
             second_half(s, 0)
             first_half(s, 1)
             zero_losers(s, 0)
-            second_half(s, 1)
             hit_back(nxt, 0)
+            second_half(s, 1)
             quantise_agg(s)
             quantise(s, 0)
             multiply_and_store(s, 0, first_rows)
@@ -495,13 +500,6 @@ def tile_stsindividuallayer_pb_v_kernel(tc, agg, W, b, pre, grad_out, out):
             multiply_and_store(s, 0, other_rows)
             reorder_grad(far)
             reorder_agg(nxt)
-            first_half(s, 2)
-            zero_losers(s, 1)
-            hit_back(nxt, 1)
-            second_half(s, 2)
-            quantise(s, 1)
-            multiply_and_store(s, 1, first_rows)
             hit_turned(far, 1, 1)
-            multiply_and_store(s, 1, other_rows)
-            zero_losers(s, last)
-            hit_back(nxt, last)
+            first_half(s, 2)
+            second_half(s, 2)

@@ -455,16 +455,18 @@ def tile_stsindividuallayer_pb_v_kernel(tc, agg, W, b, pre, grad_out, out):
             share_grad(s)
             if s >= FIRST_ON_GPSIMD:
                 share_grad_times_top(s)
-            zero_losers(s - 1, 1)
-            hit_back(s, 1)
-            zero_losers(s - 1, last)
-            hit_back(s, last)
+            if s < SLABS:
+                zero_losers(s - 1, 1)
+                hit_back(s, 1)
+                zero_losers(s - 1, last)
+                hit_back(s, last)
             if s < FIRST_ON_GPSIMD:
                 share_grad_times_top(s)
             if nxt == on_vector:
                 find_hit(nxt, 1)
             gate_product(far, 1)
-            quantise(s - 1, 1)
+            if s < SLABS:
+                quantise(s - 1, 1)
             first_max(far)
             quantise(s - 1, last)
             gate_product(far, 2)
@@ -472,10 +474,12 @@ def tile_stsindividuallayer_pb_v_kernel(tc, agg, W, b, pre, grad_out, out):
             second_max(far)
             convert_and_load(far + 1, 0)
             hit_turned(nxt, last, 0)
-            multiply_and_store(s - 1, 1, first_rows)
+            if s < SLABS:
+                multiply_and_store(s - 1, 1, first_rows)
             hit_turned(nxt, last, 1)
             negate_top(far)
-            multiply_and_store(s - 1, 1, other_rows)
+            if s < SLABS:
+                multiply_and_store(s - 1, 1, other_rows)
             count_turned(nxt, 0)
             multiply_and_store(s - 1, last, first_rows)
             count_turned(nxt, 1)
@@ -502,4 +506,11 @@ def tile_stsindividuallayer_pb_v_kernel(tc, agg, W, b, pre, grad_out, out):
             reorder_agg(nxt)
             hit_turned(far, 1, 1)
             first_half(s, 2)
+            if s == SLABS - 1:
+                zero_losers(s, 1)
             second_half(s, 2)
+            if s == SLABS - 1:
+                quantise(s, 1)
+                multiply_and_store(s, 1, first_rows)
+                multiply_and_store(s, 1, other_rows)
+                zero_losers(s, last)

@@ -31,7 +31,7 @@ BANKS_A_SLAB = SLAB_COLS // BANK
 TURNS_A_BANK = BANK // P
 TURNS_A_SLAB = SLAB_COLS // P
 GAP_SCALE = 2.0 ** 100
-FIRST_ON_GPSIMD = 2
+FIRST_ON_GPSIMD = 1
 
 FLOPS = 2 * WINDOWS * BRANCHES * NODES * CHANNELS * 2 * CHANNELS
 BYTES = WINDOWS * NODES * CHANNELS * (2 + 2) + 2 * WINDOWS * BRANCHES * NODES * 2 * CHANNELS * 4
@@ -306,6 +306,17 @@ def tile_stsindividuallayer_pb_v_kernel(tc, agg, W, b, pre, grad_out, out):
                 scale=TIE_SLOPE,
             )
 
+        def turn_hit(s, f):
+            if not live(s):
+                return
+            turning = psum_gap.tile([P, SLAB_COLS], BF16, tag="turn")
+            for turn in range(TURNS_A_SLAB):
+                cols = slice(turn * P, (turn + 1) * P)
+                nc.tensor.transpose(turning[:, cols], hit_of[s, f][:, cols], ident_bf16[:])
+            hit_t = turned.tile([P, SLAB_COLS], BF16)
+            nc.scalar.copy(out=hit_t[:], in_=turning[:])
+            hit_t_of[s, f] = hit_t
+
         def turn_hit_back(s, f):
             if not live(s):
                 return
@@ -438,7 +449,7 @@ def tile_stsindividuallayer_pb_v_kernel(tc, agg, W, b, pre, grad_out, out):
                 count_turning_back(s, bank)
 
         def hit_back(s, f):
-            if turned_path(s):
+            if turned_path(s) or (s == on_vector and f > 0):
                 turn_hit_back(s, f)
 
         first_rows = range(0, M_TILES // 2)
@@ -489,6 +500,8 @@ def tile_stsindividuallayer_pb_v_kernel(tc, agg, W, b, pre, grad_out, out):
                 find_hit(nxt, 2)
                 count_first_two(nxt)
                 count_all(nxt)
+                turn_hit(nxt, 1)
+                turn_hit(nxt, last)
             hit_turned(far, 0, 0)
             convert_and_load(far + 1, 2)
             hit_turned(far, 0, 1)

@@ -25,6 +25,7 @@ N_PASS = 2 * BLOCK
 M_TILE = 128
 M_TILES = CHANNELS // M_TILE
 RUN = 4
+PAIR = 2
 SLAB_COLS = BLOCK * PACK
 BANK = 512
 BANKS_A_SLAB = SLAB_COLS // BANK
@@ -42,12 +43,12 @@ TIE_SHIFT = -0.75 * TIE_ROOT
 TIE_OFFSET = 1.0 / 3.0
 
 
-def rows_in_runs(rows):
-    return rows.rearrange("p j (c i) -> p c j i", i=RUN)
+def rows_in_runs(rows, run=RUN):
+    return rows.rearrange("p j (c i) -> p c j i", i=run)
 
 
-def words_in_runs(words):
-    return words.rearrange("p (c i) j -> p c j i", i=RUN)
+def words_in_runs(words, run=RUN):
+    return words.rearrange("p (c i) j -> p c j i", i=run)
 
 
 def flat(words):
@@ -178,9 +179,9 @@ def tile_stsindividuallayer_pb_v_kernel(tc, agg, W, b, pre, grad_out, out):
                 return
             glu = products.tile([P, BLOCK, PACK], F32)
             nc.vector.tensor_tensor(
-                out=glu[:],
-                in0=lhs_rows_of[s, f][:].rearrange("p j c -> p c j"),
-                in1=sg_of[s, f][:],
+                out=words_in_runs(glu[:], PAIR),
+                in0=rows_in_runs(lhs_rows_of[s, f][:], PAIR),
+                in1=words_in_runs(sg_of[s, f][:], PAIR),
                 op=ALU.mult,
             )
             glu_of[s, f] = glu

@@ -31,6 +31,7 @@ BANK = 512
 BANKS_A_SLAB = SLAB_COLS // BANK
 TURNS_A_BANK = BANK // P
 TURNS_A_SLAB = SLAB_COLS // P
+PAIR_SHAPE = [P, BLOCK // PAIR, PACK, PAIR]
 GAP_SCALE = 2.0 ** 100
 FIRST_ON_GPSIMD = 1
 
@@ -53,6 +54,10 @@ def words_in_runs(words, run=RUN):
 
 def flat(words):
     return words.rearrange("p c j -> p (c j)")
+
+
+def line(pairs):
+    return pairs.rearrange("p c j i -> p (c j i)")
 
 
 def tile_stsindividuallayer_pb_v_kernel(tc, agg, W, b, pre, grad_out, out):
@@ -85,6 +90,13 @@ def tile_stsindividuallayer_pb_v_kernel(tc, agg, W, b, pre, grad_out, out):
         make_identity(nc, ident_f32[:])
         ident_bf16 = keep.tile([P, P], BF16)
         make_identity(nc, ident_bf16[:])
+        pairs_to_words = keep.tile([P, P], BF16)
+        nc.vector.tensor_copy(
+            out=pairs_to_words[:].rearrange("p (c i j) -> p c i j", i=PAIR, j=PACK),
+            in_=ident_bf16[:].rearrange("p (c j i) -> p c i j", i=PAIR, j=PACK),
+        )
+
+        on_vector = 0
 
         neg_top_of = {}
         hit_t_of = {}
@@ -177,9 +189,9 @@ def tile_stsindividuallayer_pb_v_kernel(tc, agg, W, b, pre, grad_out, out):
         def gate_product(s, f):
             if not live(s):
                 return
-            glu = products.tile([P, BLOCK, PACK], F32)
+            glu = products.tile(PAIR_SHAPE, F32)
             nc.vector.tensor_tensor(
-                out=words_in_runs(glu[:], PAIR),
+                out=glu[:],
                 in0=rows_in_runs(lhs_rows_of[s, f][:], PAIR),
                 in1=words_in_runs(sg_of[s, f][:], PAIR),
                 op=ALU.mult,
@@ -189,7 +201,7 @@ def tile_stsindividuallayer_pb_v_kernel(tc, agg, W, b, pre, grad_out, out):
         def first_max(s):
             if not live(s):
                 return
-            top01 = once.tile([P, BLOCK, PACK], F32)
+            top01 = once.tile(PAIR_SHAPE, F32)
             nc.vector.tensor_tensor(
                 out=top01[:], in0=glu_of[s, 0][:], in1=glu_of[s, 1][:], op=ALU.max
             )
@@ -198,7 +210,7 @@ def tile_stsindividuallayer_pb_v_kernel(tc, agg, W, b, pre, grad_out, out):
         def second_max(s):
             if not live(s):
                 return
-            top = pairs2.tile([P, BLOCK, PACK], F32)
+            top = pairs2.tile(PAIR_SHAPE, F32)
             nc.vector.tensor_tensor(
                 out=top[:], in0=top01_of[s][:], in1=glu_of[s, 2][:], op=ALU.max
             )
@@ -209,7 +221,10 @@ def tile_stsindividuallayer_pb_v_kernel(tc, agg, W, b, pre, grad_out, out):
                 return
             hit = flags.tile([P, BLOCK, PACK], BF16)
             nc.vector.tensor_tensor(
-                out=hit[:], in0=glu_of[s, f][:], in1=top_of[s][:], op=ALU.is_equal
+                out=words_in_runs(hit[:], PAIR),
+                in0=glu_of[s, f][:],
+                in1=top_of[s][:],
+                op=ALU.is_equal,
             )
             hit_of[s, f] = flat(hit[:])
 
@@ -242,10 +257,8 @@ def tile_stsindividuallayer_pb_v_kernel(tc, agg, W, b, pre, grad_out, out):
         def negate_top(s):
             if not live(s):
                 return
-            neg_top = thrice.tile([P, SLAB_COLS], F32)
-            nc.scalar.activation(
-                out=neg_top[:], in_=flat(top_of[s][:]), func=ACT.Copy, scale=-1.0
-            )
+            neg_top = thrice.tile(PAIR_SHAPE, F32)
+            nc.scalar.activation(out=neg_top[:], in_=top_of[s][:], func=ACT.Copy, scale=-1.0)
             neg_top_of[s] = neg_top
 
         def find_hit_turned(s, f, bank):
@@ -260,7 +273,7 @@ def tile_stsindividuallayer_pb_v_kernel(tc, agg, W, b, pre, grad_out, out):
                 here = gap_t[:, turn * P : (turn + 1) * P]
                 nc.tensor.matmul(
                     out=here,
-                    lhsT=flat(glu_of[s, f][:])[:, cols],
+                    lhsT=line(glu_of[s, f][:])[:, cols],
                     rhs=ident_f32[:],
                     is_transpose=True,
                     start=True,
@@ -268,7 +281,7 @@ def tile_stsindividuallayer_pb_v_kernel(tc, agg, W, b, pre, grad_out, out):
                 )
                 nc.tensor.matmul(
                     out=here,
-                    lhsT=neg_top_of[s][:, cols],
+                    lhsT=line(neg_top_of[s][:])[:, cols],
                     rhs=ident_f32[:],
                     is_transpose=True,
                     start=False,
@@ -295,7 +308,7 @@ def tile_stsindividuallayer_pb_v_kernel(tc, agg, W, b, pre, grad_out, out):
                     nc.tensor.matmul(
                         out=count[:, turn * P : (turn + 1) * P],
                         lhsT=hit_t_of[s, f][:, cols],
-                        rhs=ident_bf16[:],
+                        rhs=pairs_to_words[:],
                         start=(f == 0),
                         stop=(f == BRANCHES - 1),
                     )
@@ -322,9 +335,10 @@ def tile_stsindividuallayer_pb_v_kernel(tc, agg, W, b, pre, grad_out, out):
             if not live(s):
                 return
             hit_back = psum_hit.tile([P, SLAB_COLS], BF16)
+            order = ident_bf16 if s == on_vector else pairs_to_words
             for turn in range(TURNS_A_SLAB):
                 cols = slice(turn * P, (turn + 1) * P)
-                nc.tensor.transpose(hit_back[:, cols], hit_t_of[s, f][:, cols], ident_bf16[:])
+                nc.tensor.transpose(hit_back[:, cols], hit_t_of[s, f][:, cols], order[:])
             hit_of[s, f] = hit_back[:]
 
         def share_grad(s):
@@ -348,9 +362,9 @@ def tile_stsindividuallayer_pb_v_kernel(tc, agg, W, b, pre, grad_out, out):
             neg_grad_top = once.tile([P, BLOCK, PACK], F32)
             engine = nc.gpsimd if s >= FIRST_ON_GPSIMD else nc.vector
             engine.tensor_tensor(
-                out=flat(neg_grad_top[:]),
-                in0=flat(grad_share_of[s][:]),
-                in1=neg_top_of[s][:],
+                out=neg_grad_top[:].rearrange("p (c i) j -> p c i j", i=PAIR),
+                in0=grad_share_of[s][:].rearrange("p (c i) j -> p c i j", i=PAIR),
+                in1=neg_top_of[s][:].rearrange("p c j i -> p c i j"),
                 op=ALU.mult,
             )
             neg_grad_top_of[s] = neg_grad_top
@@ -431,7 +445,6 @@ def tile_stsindividuallayer_pb_v_kernel(tc, agg, W, b, pre, grad_out, out):
                 )
 
         last = BRANCHES - 1
-        on_vector = 0
 
         def turned_path(s):
             return live(s) and s != on_vector

@@ -65,23 +65,23 @@ def tile_stsindividuallayer_pb_v_kernel(tc, agg, W, b, pre, grad_out, out):
     with ExitStack() as ctx:
         keep = ctx.enter_context(tc.tile_pool(name="keep", bufs=1))
         raw = ctx.enter_context(tc.tile_pool(name="raw", bufs=BRANCHES))
-        raw_lhs = ctx.enter_context(tc.tile_pool(name="raw_lhs", bufs=2 * BRANCHES))
-        words = ctx.enter_context(tc.tile_pool(name="words", bufs=4 * BRANCHES))
-        products = ctx.enter_context(tc.tile_pool(name="products", bufs=2 * BRANCHES))
-        flags = ctx.enter_context(tc.tile_pool(name="flags", bufs=BRANCHES))
+        raw_lhs = ctx.enter_context(tc.tile_pool(name="raw_lhs", bufs=5))
+        words = ctx.enter_context(tc.tile_pool(name="words", bufs=4))
+        products = ctx.enter_context(tc.tile_pool(name="products", bufs=2))
+        flags = ctx.enter_context(tc.tile_pool(name="flags", bufs=1))
         once = ctx.enter_context(tc.tile_pool(name="once", bufs=1))
         pairs2 = ctx.enter_context(tc.tile_pool(name="pairs2", bufs=2))
         thrice = ctx.enter_context(tc.tile_pool(name="thrice", bufs=3))
-        branch = ctx.enter_context(tc.tile_pool(name="branch", bufs=BRANCHES))
+        products_bf16 = ctx.enter_context(tc.tile_pool(name="products_bf16", bufs=1))
+        results = ctx.enter_context(tc.tile_pool(name="results", bufs=2))
+        rows = ctx.enter_context(tc.tile_pool(name="rows", bufs=1))
         turned = ctx.enter_context(tc.tile_pool(name="turned", bufs=2 * BRANCHES))
-        stage = ctx.enter_context(tc.tile_pool(name="stage", bufs=6))
-        psum = ctx.enter_context(tc.psum_pool(name="psum", bufs=2))
+        stage = ctx.enter_context(tc.tile_pool(name="stage", bufs=8))
+        psum = ctx.enter_context(tc.psum_pool(name="psum", bufs=3))
         psum_gap = ctx.enter_context(tc.psum_pool(name="psum_gap", bufs=3))
-        psum_hit = ctx.enter_context(tc.psum_pool(name="psum_hit", bufs=BRANCHES))
+        psum_hit = ctx.enter_context(tc.psum_pool(name="psum_hit", bufs=2))
         ctx.enter_context(tc.manual_schedule())
 
-        agg_rows = keep.tile([P, WINDOWS, PACK, CHANNELS], BF16)
-        grad_rows = keep.tile([P, WINDOWS, PACK, CHANNELS], BF16)
         grad_words = keep.tile([P, WINDOWS, CHANNELS, PACK], BF16)
         agg_codes = keep.tile([P, WINDOWS, CHANNELS], U32, align_bytes=64)
         agg_scales = keep.tile([P, WINDOWS, CHANNELS], U8, align_bytes=64)
@@ -98,12 +98,15 @@ def tile_stsindividuallayer_pb_v_kernel(tc, agg, W, b, pre, grad_out, out):
 
         on_vector = 0
 
+        grad_rows_of = {}
+        agg_rows_of = {}
         neg_top_of = {}
         hit_t_of = {}
         rhs_rows_of = {}
         lhs_rows_of = {}
         sg_of = {}
         glu_of = {}
+        own_hits_of = {}
         hit_of = {}
         top01_of = {}
         top_of = {}
@@ -145,35 +148,42 @@ def tile_stsindividuallayer_pb_v_kernel(tc, agg, W, b, pre, grad_out, out):
             nc.sync.dma_start(out=lhs_rows[:], in_=pre_rows[:, :, c0 : c0 + BLOCK])
             lhs_rows_of[s, f] = lhs_rows
             if f == BRANCHES - 1 and s % BLOCKS == 0:
+                grad_rows = rows.tile([P, PACK, CHANNELS], BF16)
                 nc.sync.dma_start(
-                    out=grad_rows[:, w], in_=grad_out[0, w].rearrange("(p j) c -> p j c", j=PACK)
+                    out=grad_rows[:], in_=grad_out[0, w].rearrange("(p j) c -> p j c", j=PACK)
                 )
+                grad_rows_of[w] = grad_rows
             if f == BRANCHES - 1 and s % BLOCKS == BLOCKS - 1:
+                agg_rows = rows.tile([P, PACK, CHANNELS], BF16)
                 nc.sync.dma_start(
-                    out=agg_rows[:, w], in_=agg[0, w].rearrange("(p j) c -> p j c", j=PACK)
+                    out=agg_rows[:], in_=agg[0, w].rearrange("(p j) c -> p j c", j=PACK)
                 )
+                agg_rows_of[w] = agg_rows
 
         def convert(s, f):
             if not live(s):
                 return
-            sg = words.tile([P, BLOCK, PACK], F32)
+            if f == 0:
+                sg = words.tile([P, BRANCHES, BLOCK, PACK], F32)
+                sg_of[s] = sg
             nc.scalar.activation(
-                out=words_in_runs(sg[:]), in_=rows_in_runs(rhs_rows_of[s, f][:]), func=ACT.Sigmoid
+                out=words_in_runs(sg_of[s][:, f]),
+                in_=rows_in_runs(rhs_rows_of[s, f][:]),
+                func=ACT.Sigmoid,
             )
-            sg_of[s, f] = sg
 
         def reorder_grad(s):
             if live(s) and s % BLOCKS == 0:
                 w = window(s)
                 nc.scalar.copy(
-                    out=words_in_runs(grad_words[:, w]), in_=rows_in_runs(grad_rows[:, w])
+                    out=words_in_runs(grad_words[:, w]), in_=rows_in_runs(grad_rows_of[w][:])
                 )
 
         def reorder_agg(s):
             if live(s) and s % BLOCKS == 0:
                 agg_words = once.tile([P, CHANNELS, PACK], BF16, align_bytes=64)
                 nc.scalar.copy(
-                    out=words_in_runs(agg_words[:]), in_=rows_in_runs(agg_rows[:, window(s)])
+                    out=words_in_runs(agg_words[:]), in_=rows_in_runs(agg_rows_of[window(s)][:])
                 )
                 agg_words_of[s] = agg_words
 
@@ -189,21 +199,22 @@ def tile_stsindividuallayer_pb_v_kernel(tc, agg, W, b, pre, grad_out, out):
         def gate_product(s, f):
             if not live(s):
                 return
-            glu = products.tile(PAIR_SHAPE, F32)
+            if f == 0:
+                glu = products.tile([P, BRANCHES] + PAIR_SHAPE[1:], F32)
+                glu_of[s] = glu
             nc.vector.tensor_tensor(
-                out=glu[:],
+                out=glu_of[s][:, f],
                 in0=rows_in_runs(lhs_rows_of[s, f][:], PAIR),
-                in1=words_in_runs(sg_of[s, f][:], PAIR),
+                in1=words_in_runs(sg_of[s][:, f], PAIR),
                 op=ALU.mult,
             )
-            glu_of[s, f] = glu
 
         def first_max(s):
             if not live(s):
                 return
             top01 = once.tile(PAIR_SHAPE, F32)
             nc.vector.tensor_tensor(
-                out=top01[:], in0=glu_of[s, 0][:], in1=glu_of[s, 1][:], op=ALU.max
+                out=top01[:], in0=glu_of[s][:, 0], in1=glu_of[s][:, 1], op=ALU.max
             )
             top01_of[s] = top01
 
@@ -212,21 +223,23 @@ def tile_stsindividuallayer_pb_v_kernel(tc, agg, W, b, pre, grad_out, out):
                 return
             top = pairs2.tile(PAIR_SHAPE, F32)
             nc.vector.tensor_tensor(
-                out=top[:], in0=top01_of[s][:], in1=glu_of[s, 2][:], op=ALU.max
+                out=top[:], in0=top01_of[s][:], in1=glu_of[s][:, 2], op=ALU.max
             )
             top_of[s] = top
 
         def find_hit(s, f):
             if not live(s):
                 return
-            hit = flags.tile([P, BLOCK, PACK], BF16)
+            if f == 0:
+                hit = flags.tile([P, BRANCHES, BLOCK, PACK], BF16)
+                own_hits_of[s] = hit
             nc.vector.tensor_tensor(
-                out=words_in_runs(hit[:], PAIR),
-                in0=glu_of[s, f][:],
+                out=words_in_runs(own_hits_of[s][:, f], PAIR),
+                in0=glu_of[s][:, f],
                 in1=top_of[s][:],
                 op=ALU.is_equal,
             )
-            hit_of[s, f] = flat(hit[:])
+            hit_of[s, f] = flat(own_hits_of[s][:, f])
 
         def count_first_two(s):
             if not live(s):
@@ -273,7 +286,7 @@ def tile_stsindividuallayer_pb_v_kernel(tc, agg, W, b, pre, grad_out, out):
                 here = gap_t[:, turn * P : (turn + 1) * P]
                 nc.tensor.matmul(
                     out=here,
-                    lhsT=line(glu_of[s, f][:])[:, cols],
+                    lhsT=line(glu_of[s][:, f])[:, cols],
                     rhs=ident_f32[:],
                     is_transpose=True,
                     start=True,
@@ -369,23 +382,37 @@ def tile_stsindividuallayer_pb_v_kernel(tc, agg, W, b, pre, grad_out, out):
             )
             neg_grad_top_of[s] = neg_grad_top
 
-        def first_half(s, f):
+        def dpre(s, f, count):
+            if f == 0:
+                return dpre_of[s, 0][:]
+            return dpre_of[s, 1][:, f - 1 : f - 1 + count]
+
+        def first_half(s, f, count):
             if not live(s):
                 return
-            dpre = branch.tile([P, N_PASS, PACK], BF16, align_bytes=64)
+            if f == 0:
+                first_dpre = products_bf16.tile([P, 1, 2, SLAB_COLS], BF16, align_bytes=64)
+                dpre_of[s, 0] = first_dpre
+            if f == 1:
+                other_dpre = products_bf16.tile(
+                    [P, BRANCHES - 1, 2, SLAB_COLS], BF16, align_bytes=64
+                )
+                dpre_of[s, 1] = other_dpre
             nc.vector.tensor_tensor(
-                out=dpre[:, 0:BLOCK, :], in0=sg_of[s, f][:], in1=grad_share_of[s][:], op=ALU.mult
+                out=dpre(s, f, count)[:, :, 0],
+                in0=sg_of[s][:, f : f + count].rearrange("p f c j -> p f (c j)"),
+                in1=flat(grad_share_of[s][:]).unsqueeze(1).to_broadcast([P, count, SLAB_COLS]),
+                op=ALU.mult,
             )
-            dpre_of[s, f] = dpre
 
-        def second_half(s, f):
+        def second_half(s, f, count):
             if not live(s):
                 return
             nc.vector.scalar_tensor_tensor(
-                out=dpre_of[s, f][:, BLOCK:N_PASS, :],
-                in0=sg_of[s, f][:],
+                out=dpre(s, f, count)[:, :, 1],
+                in0=sg_of[s][:, f : f + count].rearrange("p f c j -> p f (c j)"),
                 scalar=1.0,
-                in1=neg_grad_top_of[s][:],
+                in1=flat(neg_grad_top_of[s][:]).unsqueeze(1).to_broadcast([P, count, SLAB_COLS]),
                 op0=ALU.subtract,
                 op1=ALU.mult,
             )
@@ -393,7 +420,7 @@ def tile_stsindividuallayer_pb_v_kernel(tc, agg, W, b, pre, grad_out, out):
         def zero_losers(s, f):
             if not live(s):
                 return
-            halves = dpre_of[s, f][:].rearrange("p (h c) j -> p h (c j)", h=2)
+            halves = dpre(s, f, 1)[:, 0]
             nc.vector.tensor_tensor(
                 out=halves,
                 in0=halves,
@@ -401,16 +428,19 @@ def tile_stsindividuallayer_pb_v_kernel(tc, agg, W, b, pre, grad_out, out):
                 op=ALU.mult,
             )
 
-        def quantise(s, f):
+        def quantise(s, f, count):
             if not live(s):
                 return
-            codes = branch.tile([P, N_PASS], U32, align_bytes=64)
-            scales = branch.tile([P, N_PASS], U8, align_bytes=64)
+            if f == 0:
+                codes = results.tile([P, BRANCHES, N_PASS], U32, align_bytes=64)
+                scales = results.tile([P, BRANCHES, N_PASS], U8, align_bytes=64)
+                codes_of[s] = codes
+                scales_of[s] = scales
             nc.vector.quantize_mx(
-                out=codes[:].bitcast(E5M2_X4), scales=scales[:], in_=flat(dpre_of[s, f][:])
+                out=codes_of[s][:, f : f + count].rearrange("p f n -> p (f n)").bitcast(E5M2_X4),
+                scales=scales_of[s][:, f : f + count].rearrange("p f n -> p (f n)"),
+                in_=dpre(s, f, count).rearrange("p f h n -> p (f h n)"),
             )
-            codes_of[s, f] = codes
-            scales_of[s, f] = scales
 
         def multiply_and_store(s, f, m_tiles):
             if not live(s):
@@ -427,8 +457,8 @@ def tile_stsindividuallayer_pb_v_kernel(tc, agg, W, b, pre, grad_out, out):
                     out=acc[:],
                     lhsT=agg_codes[:, w, m_cols].bitcast(E4M3_X4),
                     lhsT_scale=agg_scales[:, w, m_cols],
-                    rhs=codes_of[s, f][:].bitcast(E5M2_X4),
-                    rhs_scale=scales_of[s, f][:],
+                    rhs=codes_of[s][:, f].bitcast(E5M2_X4),
+                    rhs_scale=scales_of[s][:, f],
                     start=True,
                     stop=True,
                 )
@@ -466,14 +496,14 @@ def tile_stsindividuallayer_pb_v_kernel(tc, agg, W, b, pre, grad_out, out):
             if turned_path(s) or (s == on_vector and f > 0):
                 turn_hit_back(s, f)
 
-        first_rows = range(0, M_TILES // 2)
-        other_rows = range(M_TILES // 2, M_TILES)
+        all_rows = range(M_TILES)
         for f in range(BRANCHES):
             load_rhs(0, f)
             load_lhs(0, f)
         for s in range(-3, SLABS + 1):
             nxt = s + 1
             far = s + 2
+            final = s == SLABS - 1
             if nxt == on_vector:
                 find_hit(nxt, 0)
             gate_product(far, 0)
@@ -482,33 +512,34 @@ def tile_stsindividuallayer_pb_v_kernel(tc, agg, W, b, pre, grad_out, out):
                 share_grad_times_top(s)
             if s < SLABS:
                 zero_losers(s - 1, 1)
-                hit_back(s, 1)
+                hit_back(s, 0)
                 zero_losers(s - 1, last)
-                hit_back(s, last)
+                hit_back(s, 1)
             if s < FIRST_ON_GPSIMD:
                 share_grad_times_top(s)
             if nxt == on_vector:
                 find_hit(nxt, 1)
             gate_product(far, 1)
+            if not live(far):
+                first_half(s, 0, 1)
             if s < SLABS:
-                quantise(s - 1, 1)
+                quantise(s - 1, 1, 2)
+            else:
+                quantise(s - 1, last, 1)
             first_max(far)
-            quantise(s - 1, last)
             gate_product(far, 2)
-            first_half(s, 0)
+            if live(far):
+                first_half(s, 0, 1)
             second_max(far)
             convert_and_load(far + 1, 0)
             hit_turned(nxt, last, 0)
-            if s < SLABS:
-                multiply_and_store(s - 1, 1, first_rows)
             hit_turned(nxt, last, 1)
             negate_top(far)
-            if s < SLABS:
-                multiply_and_store(s - 1, 1, other_rows)
             count_turned(nxt, 0)
-            multiply_and_store(s - 1, last, first_rows)
             count_turned(nxt, 1)
-            multiply_and_store(s - 1, last, other_rows)
+            if s < SLABS:
+                multiply_and_store(s - 1, 1, all_rows)
+            multiply_and_store(s - 1, last, all_rows)
             convert_and_load(far + 1, 1)
             if nxt == on_vector:
                 find_hit(nxt, 2)
@@ -519,25 +550,22 @@ def tile_stsindividuallayer_pb_v_kernel(tc, agg, W, b, pre, grad_out, out):
             hit_turned(far, 0, 0)
             convert_and_load(far + 1, 2)
             hit_turned(far, 0, 1)
-            second_half(s, 0)
-            first_half(s, 1)
+            second_half(s, 0, 1)
+            first_half(s, 1, 1 if final else 2)
             zero_losers(s, 0)
-            hit_back(nxt, 0)
-            second_half(s, 1)
+            hit_back(s, last)
+            second_half(s, 1, 1 if final else 2)
             quantise_agg(s)
-            quantise(s, 0)
-            multiply_and_store(s, 0, first_rows)
+            quantise(s, 0, 1)
+            multiply_and_store(s, 0, all_rows)
             hit_turned(far, 1, 0)
-            multiply_and_store(s, 0, other_rows)
             reorder_grad(far)
             reorder_agg(nxt)
             hit_turned(far, 1, 1)
-            first_half(s, 2)
-            if s == SLABS - 1:
+            if final:
                 zero_losers(s, 1)
-            second_half(s, 2)
-            if s == SLABS - 1:
-                quantise(s, 1)
-                multiply_and_store(s, 1, first_rows)
-                multiply_and_store(s, 1, other_rows)
+                first_half(s, last, 1)
+                quantise(s, 1, 1)
+                multiply_and_store(s, 1, all_rows)
+                second_half(s, last, 1)
                 zero_losers(s, last)

@@ -65,7 +65,7 @@ def tile_stsindividuallayer_pb_v_kernel(tc, agg, W, b, pre, grad_out, out):
     with ExitStack() as ctx:
         keep = ctx.enter_context(tc.tile_pool(name="keep", bufs=1))
         raw = ctx.enter_context(tc.tile_pool(name="raw", bufs=BRANCHES))
-        raw_lhs = ctx.enter_context(tc.tile_pool(name="raw_lhs", bufs=5))
+        raw_lhs = ctx.enter_context(tc.tile_pool(name="raw_lhs", bufs=4))
         words = ctx.enter_context(tc.tile_pool(name="words", bufs=4))
         products = ctx.enter_context(tc.tile_pool(name="products", bufs=2))
         flags = ctx.enter_context(tc.tile_pool(name="flags", bufs=1))
@@ -75,11 +75,12 @@ def tile_stsindividuallayer_pb_v_kernel(tc, agg, W, b, pre, grad_out, out):
         products_bf16 = ctx.enter_context(tc.tile_pool(name="products_bf16", bufs=1))
         results = ctx.enter_context(tc.tile_pool(name="results", bufs=2))
         rows = ctx.enter_context(tc.tile_pool(name="rows", bufs=1))
+        rows2 = ctx.enter_context(tc.tile_pool(name="rows2", bufs=WINDOWS))
         turned = ctx.enter_context(tc.tile_pool(name="turned", bufs=2 * BRANCHES))
         stage = ctx.enter_context(tc.tile_pool(name="stage", bufs=8))
-        psum = ctx.enter_context(tc.psum_pool(name="psum", bufs=3))
+        psum = ctx.enter_context(tc.psum_pool(name="psum", bufs=2))
         psum_gap = ctx.enter_context(tc.psum_pool(name="psum_gap", bufs=3))
-        psum_hit = ctx.enter_context(tc.psum_pool(name="psum_hit", bufs=2))
+        psum_hit = ctx.enter_context(tc.psum_pool(name="psum_hit", bufs=BRANCHES))
         ctx.enter_context(tc.manual_schedule())
 
         grad_words = keep.tile([P, WINDOWS, CHANNELS, PACK], BF16)
@@ -153,8 +154,9 @@ def tile_stsindividuallayer_pb_v_kernel(tc, agg, W, b, pre, grad_out, out):
                     out=grad_rows[:], in_=grad_out[0, w].rearrange("(p j) c -> p j c", j=PACK)
                 )
                 grad_rows_of[w] = grad_rows
-            if f == BRANCHES - 1 and s % BLOCKS == BLOCKS - 1:
-                agg_rows = rows.tile([P, PACK, CHANNELS], BF16)
+            if f == BRANCHES - 1 and s in (1, 2):
+                w = s - 1
+                agg_rows = rows2.tile([P, PACK, CHANNELS], BF16)
                 nc.sync.dma_start(
                     out=agg_rows[:], in_=agg[0, w].rearrange("(p j) c -> p j c", j=PACK)
                 )
@@ -230,7 +232,7 @@ def tile_stsindividuallayer_pb_v_kernel(tc, agg, W, b, pre, grad_out, out):
         def find_hit(s, f):
             if not live(s):
                 return
-            if f == 0:
+            if s not in own_hits_of:
                 hit = flags.tile([P, BRANCHES, BLOCK, PACK], BF16)
                 own_hits_of[s] = hit
             nc.vector.tensor_tensor(
@@ -500,26 +502,61 @@ def tile_stsindividuallayer_pb_v_kernel(tc, agg, W, b, pre, grad_out, out):
         for f in range(BRANCHES):
             load_rhs(0, f)
             load_lhs(0, f)
-        for s in range(-3, SLABS + 1):
+        for f in range(BRANCHES):
+            convert_and_load(0, f)
+        gate_product(0, 0)
+        gate_product(0, 1)
+        first_max(0)
+        gate_product(0, 2)
+        second_max(0)
+        reorder_grad(0)
+        convert_and_load(1, 0)
+        negate_top(0)
+        convert_and_load(1, 1)
+        find_hit(0, 1)
+        find_hit(0, 2)
+        find_hit(0, 0)
+        count_first_two(0)
+        count_all(0)
+        turn_hit(0, 1)
+        turn_hit(0, last)
+        turn_hit_back(0, 1)
+        turn_hit_back(0, last)
+        convert_and_load(1, 2)
+        gate_product(1, 0)
+        share_grad(0)
+        gate_product(1, 1)
+        share_grad_times_top(0)
+        first_max(1)
+        gate_product(1, 2)
+        convert_and_load(2, 0)
+        second_max(1)
+        negate_top(1)
+        convert_and_load(2, 1)
+        hit_turned(1, 0, 0)
+        hit_turned(1, 0, 1)
+        convert_and_load(2, 2)
+        hit_turned(1, 1, 0)
+        reorder_agg(0)
+        hit_turned(1, 1, 1)
+        for s in range(SLABS + 1):
             nxt = s + 1
             far = s + 2
             final = s == SLABS - 1
-            if nxt == on_vector:
-                find_hit(nxt, 0)
             gate_product(far, 0)
-            share_grad(s)
-            if s >= FIRST_ON_GPSIMD:
+            if s > 0:
+                share_grad(s)
                 share_grad_times_top(s)
-            if s < SLABS:
+            if 0 < s < SLABS:
                 zero_losers(s - 1, 1)
-                hit_back(s, 0)
-                zero_losers(s - 1, last)
                 hit_back(s, 1)
-            if s < FIRST_ON_GPSIMD:
-                share_grad_times_top(s)
-            if nxt == on_vector:
-                find_hit(nxt, 1)
+                zero_losers(s - 1, last)
+                hit_back(s, last)
+            if s == 0:
+                first_half(s, 0, 1)
             gate_product(far, 1)
+            if s == 0:
+                second_half(s, 0, 1)
             if not live(far):
                 first_half(s, 0, 1)
             if s < SLABS:
@@ -527,9 +564,13 @@ def tile_stsindividuallayer_pb_v_kernel(tc, agg, W, b, pre, grad_out, out):
             else:
                 quantise(s - 1, last, 1)
             first_max(far)
+            if s == 0:
+                first_half(s, 1, 2)
             gate_product(far, 2)
-            if live(far):
+            if s > 0 and live(far):
                 first_half(s, 0, 1)
+            if s == 0:
+                zero_losers(s, 0)
             second_max(far)
             convert_and_load(far + 1, 0)
             hit_turned(nxt, last, 0)
@@ -541,26 +582,22 @@ def tile_stsindividuallayer_pb_v_kernel(tc, agg, W, b, pre, grad_out, out):
                 multiply_and_store(s - 1, 1, all_rows)
             multiply_and_store(s - 1, last, all_rows)
             convert_and_load(far + 1, 1)
-            if nxt == on_vector:
-                find_hit(nxt, 2)
-                count_first_two(nxt)
-                count_all(nxt)
-                turn_hit(nxt, 1)
-                turn_hit(nxt, last)
             hit_turned(far, 0, 0)
             convert_and_load(far + 1, 2)
             hit_turned(far, 0, 1)
-            second_half(s, 0, 1)
-            first_half(s, 1, 1 if final else 2)
-            zero_losers(s, 0)
-            hit_back(s, last)
+            if s > 0:
+                second_half(s, 0, 1)
+                first_half(s, 1, 1 if final else 2)
+                zero_losers(s, 0)
+            hit_back(nxt, 0)
             second_half(s, 1, 1 if final else 2)
             quantise_agg(s)
             quantise(s, 0, 1)
             multiply_and_store(s, 0, all_rows)
+            if s % BLOCKS == 0:
+                reorder_agg(s + BLOCKS)
             hit_turned(far, 1, 0)
             reorder_grad(far)
-            reorder_agg(nxt)
             hit_turned(far, 1, 1)
             if final:
                 zero_losers(s, 1)

@@ -78,9 +78,9 @@ def tile_stsindividuallayer_pb_v_kernel(tc, agg, W, b, pre, grad_out, out):
         rows2 = ctx.enter_context(tc.tile_pool(name="rows2", bufs=WINDOWS))
         turned = ctx.enter_context(tc.tile_pool(name="turned", bufs=2 * BRANCHES))
         stage = ctx.enter_context(tc.tile_pool(name="stage", bufs=8))
-        psum = ctx.enter_context(tc.psum_pool(name="psum", bufs=2))
+        psum = ctx.enter_context(tc.psum_pool(name="psum", bufs=3))
         psum_gap = ctx.enter_context(tc.psum_pool(name="psum_gap", bufs=3))
-        psum_hit = ctx.enter_context(tc.psum_pool(name="psum_hit", bufs=BRANCHES))
+        psum_hit = ctx.enter_context(tc.psum_pool(name="psum_hit", bufs=2))
         ctx.enter_context(tc.manual_schedule())
 
         grad_words = keep.tile([P, WINDOWS, CHANNELS, PACK], BF16)
@@ -549,9 +549,9 @@ def tile_stsindividuallayer_pb_v_kernel(tc, agg, W, b, pre, grad_out, out):
                 share_grad_times_top(s)
             if 0 < s < SLABS:
                 zero_losers(s - 1, 1)
-                hit_back(s, 1)
+                hit_back(s, 0)
                 zero_losers(s - 1, last)
-                hit_back(s, last)
+                hit_back(s, 1)
             if s == 0:
                 first_half(s, 0, 1)
             gate_product(far, 1)
@@ -573,13 +573,27 @@ def tile_stsindividuallayer_pb_v_kernel(tc, agg, W, b, pre, grad_out, out):
                 zero_losers(s, 0)
             second_max(far)
             convert_and_load(far + 1, 0)
-            hit_turned(nxt, last, 0)
-            hit_turned(nxt, last, 1)
-            negate_top(far)
-            count_turned(nxt, 0)
-            count_turned(nxt, 1)
+            if s == 1:
+                hit_turned(nxt, last, 0)
+                hit_turned(nxt, last, 1)
+                negate_top(far)
+                count_turned(nxt, 0)
+                count_turned(nxt, 1)
+            if s == 2:
+                hit_turned(nxt, last, 0)
+                negate_top(far)
+            if s not in (1, 2):
+                hit_turned(nxt, last, 0)
+                hit_turned(nxt, last, 1)
+                negate_top(far)
+                count_turned(nxt, 0)
+                count_turned(nxt, 1)
             if s < SLABS:
                 multiply_and_store(s - 1, 1, all_rows)
+            if s == 2:
+                hit_turned(nxt, last, 1)
+                count_turned(nxt, 0)
+                count_turned(nxt, 1)
             multiply_and_store(s - 1, last, all_rows)
             convert_and_load(far + 1, 1)
             hit_turned(far, 0, 0)
@@ -589,7 +603,7 @@ def tile_stsindividuallayer_pb_v_kernel(tc, agg, W, b, pre, grad_out, out):
                 second_half(s, 0, 1)
                 first_half(s, 1, 1 if final else 2)
                 zero_losers(s, 0)
-            hit_back(nxt, 0)
+                hit_back(s, last)
             second_half(s, 1, 1 if final else 2)
             quantise_agg(s)
             quantise(s, 0, 1)

@@ -169,8 +169,8 @@ def tile_stsindividuallayer_pb_v_kernel(tc, agg, W, b, pre, grad_out, out):
                 sg = words.tile([P, BRANCHES, BLOCK, PACK], F32)
                 sg_of[s] = sg
             nc.scalar.activation(
-                out=words_in_runs(sg_of[s][:, f]),
-                in_=rows_in_runs(rhs_rows_of[s, f][:]),
+                out=words_in_runs(sg_of[s][:, f], PAIR),
+                in_=rows_in_runs(rhs_rows_of[s, f][:], PAIR),
                 func=ACT.Sigmoid,
             )
 
@@ -338,22 +338,33 @@ def tile_stsindividuallayer_pb_v_kernel(tc, agg, W, b, pre, grad_out, out):
         def turn_hit(s, f):
             if not live(s):
                 return
-            turning = psum_gap.tile([P, SLAB_COLS], BF16, tag="turn")
-            for turn in range(TURNS_A_SLAB):
+            turning = psum_gap.tile([P, BANK], F32, tag="turn")
+            for turn in range(TURNS_A_BANK):
                 cols = slice(turn * P, (turn + 1) * P)
-                nc.tensor.transpose(turning[:, cols], hit_of[s, f][:, cols], ident_bf16[:])
-            hit_t = turned.tile([P, SLAB_COLS], BF16)
-            nc.scalar.copy(out=hit_t[:], in_=turning[:])
-            hit_t_of[s, f] = hit_t
+                nc.tensor.transpose(
+                    turning[:, cols], hit_of[s, f].bitcast(F32)[:, cols], ident_f32[:]
+                )
+            hit_words = turned.tile([P, BANK], F32, tag="hit_t")
+            nc.scalar.copy(out=hit_words[:], in_=turning[:])
+            hit_t_of[s, f] = hit_words
 
         def turn_hit_back(s, f):
             if not live(s):
                 return
             hit_back = psum_hit.tile([P, SLAB_COLS], BF16)
-            order = ident_bf16 if s == on_vector else pairs_to_words
-            for turn in range(TURNS_A_SLAB):
-                cols = slice(turn * P, (turn + 1) * P)
-                nc.tensor.transpose(hit_back[:, cols], hit_t_of[s, f][:, cols], order[:])
+            if s == on_vector:
+                words_back = hit_back[:].bitcast(F32)
+                for turn in range(TURNS_A_BANK):
+                    cols = slice(turn * P, (turn + 1) * P)
+                    nc.tensor.transpose(
+                        words_back[:, cols], hit_t_of[s, f][:, cols], ident_f32[:]
+                    )
+            else:
+                for turn in range(TURNS_A_SLAB):
+                    cols = slice(turn * P, (turn + 1) * P)
+                    nc.tensor.transpose(
+                        hit_back[:, cols], hit_t_of[s, f][:, cols], pairs_to_words[:]
+                    )
             hit_of[s, f] = hit_back[:]
 
         def share_grad(s):
@@ -514,8 +525,8 @@ def tile_stsindividuallayer_pb_v_kernel(tc, agg, W, b, pre, grad_out, out):
         negate_top(0)
         convert_and_load(1, 1)
         find_hit(0, 1)
-        find_hit(0, 2)
         find_hit(0, 0)
+        find_hit(0, 2)
         count_first_two(0)
         count_all(0)
         turn_hit(0, 1)
@@ -524,13 +535,13 @@ def tile_stsindividuallayer_pb_v_kernel(tc, agg, W, b, pre, grad_out, out):
         turn_hit_back(0, last)
         convert_and_load(1, 2)
         gate_product(1, 0)
-        share_grad(0)
         gate_product(1, 1)
-        share_grad_times_top(0)
+        share_grad(0)
         first_max(1)
         gate_product(1, 2)
-        convert_and_load(2, 0)
+        share_grad_times_top(0)
         second_max(1)
+        convert_and_load(2, 0)
         negate_top(1)
         convert_and_load(2, 1)
         hit_turned(1, 0, 0)
@@ -559,8 +570,11 @@ def tile_stsindividuallayer_pb_v_kernel(tc, agg, W, b, pre, grad_out, out):
                 second_half(s, 0, 1)
             if not live(far):
                 first_half(s, 0, 1)
-            if s < SLABS:
+            if s < SLABS - 1:
                 quantise(s - 1, 1, 2)
+            elif final:
+                quantise(s - 1, 1, 1)
+                quantise(s - 1, last, 1)
             else:
                 quantise(s - 1, last, 1)
             first_max(far)
@@ -573,6 +587,12 @@ def tile_stsindividuallayer_pb_v_kernel(tc, agg, W, b, pre, grad_out, out):
                 zero_losers(s, 0)
             second_max(far)
             convert_and_load(far + 1, 0)
+            if s == 0:
+                hit_turned(nxt, last, 0)
+                hit_turned(nxt, last, 1)
+                negate_top(far)
+                count_turned(nxt, 0)
+                count_turned(nxt, 1)
             if s == 1:
                 hit_turned(nxt, last, 0)
                 hit_turned(nxt, last, 1)
@@ -582,7 +602,7 @@ def tile_stsindividuallayer_pb_v_kernel(tc, agg, W, b, pre, grad_out, out):
             if s == 2:
                 hit_turned(nxt, last, 0)
                 negate_top(far)
-            if s not in (1, 2):
+            if s > 2:
                 hit_turned(nxt, last, 0)
                 hit_turned(nxt, last, 1)
                 negate_top(far)

@@ -545,8 +545,8 @@ def tile_stsindividuallayer_pb_v_kernel(tc, agg, W, b, pre, grad_out, out):
         negate_top(1)
         convert_and_load(2, 1)
         hit_turned(1, 0, 0)
-        hit_turned(1, 0, 1)
         convert_and_load(2, 2)
+        hit_turned(1, 0, 1)
         hit_turned(1, 1, 0)
         reorder_agg(0)
         hit_turned(1, 1, 1)
@@ -627,10 +627,11 @@ def tile_stsindividuallayer_pb_v_kernel(tc, agg, W, b, pre, grad_out, out):
             second_half(s, 1, 1 if final else 2)
             quantise_agg(s)
             quantise(s, 0, 1)
-            multiply_and_store(s, 0, all_rows)
+            multiply_and_store(s, 0, range(2))
+            hit_turned(far, 1, 0)
+            multiply_and_store(s, 0, range(2, 4))
             if s % BLOCKS == 0:
                 reorder_agg(s + BLOCKS)
-            hit_turned(far, 1, 0)
             reorder_grad(far)
             hit_turned(far, 1, 1)
             if final:

from contextlib import ExitStack

import concourse.mybir as mybir
from concourse.masks import make_identity

F32 = mybir.dt.float32
BF16 = mybir.dt.bfloat16
U32 = mybir.dt.uint32
U8 = mybir.dt.uint8
E4M3_X4 = mybir.dt.float8_e4m3fn_x4
E5M2_X4 = mybir.dt.float8_e5m2_x4
ALU = mybir.AluOpType
ACT = mybir.ActivationFunctionType

P = 128
PACK = 4
WINDOWS = 2
BRANCHES = 3
NODES = P * PACK
CHANNELS = 512
BLOCK = 256
BLOCKS = CHANNELS // BLOCK
SLABS = WINDOWS * BLOCKS
N_PASS = 2 * BLOCK
M_TILE = 128
M_TILES = CHANNELS // M_TILE
RUN = 4
PAIR = 2
SLAB_COLS = BLOCK * PACK
BANK = 512
BANKS_A_SLAB = SLAB_COLS // BANK
TURNS_A_BANK = BANK // P
TURNS_A_SLAB = SLAB_COLS // P
PAIR_SHAPE = [P, BLOCK // PAIR, PACK, PAIR]
GAP_SCALE = 2.0 ** 100
FIRST_ON_GPSIMD = 1

FLOPS = 2 * WINDOWS * BRANCHES * NODES * CHANNELS * 2 * CHANNELS
BYTES = WINDOWS * NODES * CHANNELS * (2 + 2) + 2 * WINDOWS * BRANCHES * NODES * 2 * CHANNELS * 4

TIE_ROOT = (8.0 / 3.0) ** 0.5
TIE_SLOPE = 0.25 * TIE_ROOT
TIE_SHIFT = -0.75 * TIE_ROOT
TIE_OFFSET = 1.0 / 3.0


def rows_in_runs(rows, run=RUN):
    return rows.rearrange("p j (c i) -> p c j i", i=run)


def words_in_runs(words, run=RUN):
    return words.rearrange("p (c i) j -> p c j i", i=run)


def flat(words):
    return words.rearrange("p c j -> p (c j)")


def line(pairs):
    return pairs.rearrange("p c j i -> p (c j i)")


def tile_stsindividuallayer_pb_v_kernel(tc, agg, W, b, pre, grad_out, out):
    nc = tc.nc
    with ExitStack() as ctx:
        keep = ctx.enter_context(tc.tile_pool(name="keep", bufs=1))
        raw = ctx.enter_context(tc.tile_pool(name="raw", bufs=BRANCHES))
        raw_lhs = ctx.enter_context(tc.tile_pool(name="raw_lhs", bufs=4))
        words = ctx.enter_context(tc.tile_pool(name="words", bufs=4))
        products = ctx.enter_context(tc.tile_pool(name="products", bufs=2))
        flags = ctx.enter_context(tc.tile_pool(name="flags", bufs=1))
        once = ctx.enter_context(tc.tile_pool(name="once", bufs=1))
        pairs2 = ctx.enter_context(tc.tile_pool(name="pairs2", bufs=2))
        thrice = ctx.enter_context(tc.tile_pool(name="thrice", bufs=3))
        products_bf16 = ctx.enter_context(tc.tile_pool(name="products_bf16", bufs=1))
        results = ctx.enter_context(tc.tile_pool(name="results", bufs=2))
        rows = ctx.enter_context(tc.tile_pool(name="rows", bufs=1))
        rows2 = ctx.enter_context(tc.tile_pool(name="rows2", bufs=WINDOWS))
        turned = ctx.enter_context(tc.tile_pool(name="turned", bufs=2 * BRANCHES))
        stage = ctx.enter_context(tc.tile_pool(name="stage", bufs=8))
        psum = ctx.enter_context(tc.psum_pool(name="psum", bufs=3))
        psum_gap = ctx.enter_context(tc.psum_pool(name="psum_gap", bufs=3))
        psum_hit = ctx.enter_context(tc.psum_pool(name="psum_hit", bufs=2))
        ctx.enter_context(tc.manual_schedule())

        grad_words = keep.tile([P, WINDOWS, CHANNELS, PACK], BF16)
        agg_codes = keep.tile([P, WINDOWS, CHANNELS], U32, align_bytes=64)
        agg_scales = keep.tile([P, WINDOWS, CHANNELS], U8, align_bytes=64)

        ident_f32 = keep.tile([P, P], F32)
        make_identity(nc, ident_f32[:])
        ident_bf16 = keep.tile([P, P], BF16)
        make_identity(nc, ident_bf16[:])
        pairs_to_words = keep.tile([P, P], BF16)
        nc.vector.tensor_copy(
            out=pairs_to_words[:].rearrange("p (c i j) -> p c i j", i=PAIR, j=PACK),
            in_=ident_bf16[:].rearrange("p (c j i) -> p c i j", i=PAIR, j=PACK),
        )

        on_vector = 0

        grad_rows_of = {}
        agg_rows_of = {}
        neg_top_of = {}
        hit_t_of = {}
        rhs_rows_of = {}
        lhs_rows_of = {}
        sg_of = {}
        glu_of = {}
        own_hits_of = {}
        hit_of = {}
        top01_of = {}
        top_of = {}
        hits01_of = {}
        tie_square_of = {}
        grad_share_of = {}
        neg_grad_top_of = {}
        dpre_of = {}
        codes_of = {}
        scales_of = {}
        agg_words_of = {}

        def live(s):
            return 0 <= s < SLABS

        def window(s):
            return s // BLOCKS

        def first_channel(s):
            return (s % BLOCKS) * BLOCK

        def load_rhs(s, f):
            if not live(s):
                return
            c0 = first_channel(s)
            pre_rows = pre[0, window(s), f].rearrange("(p j) n -> p j n", j=PACK)
            rhs_rows = raw.tile([P, PACK, BLOCK], F32)
            nc.sync.dma_start(
                out=rhs_rows[:], in_=pre_rows[:, :, CHANNELS + c0 : CHANNELS + c0 + BLOCK]
            )
            rhs_rows_of[s, f] = rhs_rows

        def load_lhs(s, f):
            if not live(s):
                return
            w, c0 = window(s), first_channel(s)
            pre_rows = pre[0, w, f].rearrange("(p j) n -> p j n", j=PACK)
            lhs_rows = raw_lhs.tile([P, PACK, BLOCK], F32)
            nc.sync.dma_start(out=lhs_rows[:], in_=pre_rows[:, :, c0 : c0 + BLOCK])
            lhs_rows_of[s, f] = lhs_rows
            if f == BRANCHES - 1 and s % BLOCKS == 0:
                grad_rows = rows.tile([P, PACK, CHANNELS], BF16)
                nc.sync.dma_start(
                    out=grad_rows[:], in_=grad_out[0, w].rearrange("(p j) c -> p j c", j=PACK)
                )
                grad_rows_of[w] = grad_rows
            if f == BRANCHES - 1 and s in (1, 2):
                w = s - 1
                agg_rows = rows2.tile([P, PACK, CHANNELS], BF16)
                nc.sync.dma_start(
                    out=agg_rows[:], in_=agg[0, w].rearrange("(p j) c -> p j c", j=PACK)
                )
                agg_rows_of[w] = agg_rows

        def convert(s, f):
            if not live(s):
                return
            if f == 0:
                sg = words.tile([P, BRANCHES, BLOCK, PACK], F32)
                sg_of[s] = sg
            nc.scalar.activation(
                out=words_in_runs(sg_of[s][:, f], PAIR),
                in_=rows_in_runs(rhs_rows_of[s, f][:], PAIR),
                func=ACT.Sigmoid,
            )

        def reorder_grad(s):
            if live(s) and s % BLOCKS == 0:
                w = window(s)
                nc.scalar.copy(
                    out=words_in_runs(grad_words[:, w]), in_=rows_in_runs(grad_rows_of[w][:])
                )

        def reorder_agg(s):
            if live(s) and s % BLOCKS == 0:
                agg_words = once.tile([P, CHANNELS, PACK], BF16, align_bytes=64)
                nc.scalar.copy(
                    out=words_in_runs(agg_words[:]), in_=rows_in_runs(agg_rows_of[window(s)][:])
                )
                agg_words_of[s] = agg_words

        def quantise_agg(s):
            if live(s) and s % BLOCKS == 0:
                w = window(s)
                nc.vector.quantize_mx(
                    out=agg_codes[:, w].bitcast(E4M3_X4),
                    scales=agg_scales[:, w],
                    in_=flat(agg_words_of[s][:]),
                )

        def gate_product(s, f):
            if not live(s):
                return
            if f == 0:
                glu = products.tile([P, BRANCHES] + PAIR_SHAPE[1:], F32)
                glu_of[s] = glu
            nc.vector.tensor_tensor(
                out=glu_of[s][:, f],
                in0=rows_in_runs(lhs_rows_of[s, f][:], PAIR),
                in1=words_in_runs(sg_of[s][:, f], PAIR),
                op=ALU.mult,
            )

        def first_max(s):
            if not live(s):
                return
            top01 = once.tile(PAIR_SHAPE, F32)
            nc.vector.tensor_tensor(
                out=top01[:], in0=glu_of[s][:, 0], in1=glu_of[s][:, 1], op=ALU.max
            )
            top01_of[s] = top01

        def second_max(s):
            if not live(s):
                return
            top = pairs2.tile(PAIR_SHAPE, F32)
            nc.vector.tensor_tensor(
                out=top[:], in0=top01_of[s][:], in1=glu_of[s][:, 2], op=ALU.max
            )
            top_of[s] = top

        def find_hit(s, f):
            if not live(s):
                return
            if s not in own_hits_of:
                hit = flags.tile([P, BRANCHES, BLOCK, PACK], BF16)
                own_hits_of[s] = hit
            nc.vector.tensor_tensor(
                out=words_in_runs(own_hits_of[s][:, f], PAIR),
                in0=glu_of[s][:, f],
                in1=top_of[s][:],
                op=ALU.is_equal,
            )
            hit_of[s, f] = flat(own_hits_of[s][:, f])

        def count_first_two(s):
            if not live(s):
                return
            hits01 = once.tile([P, BLOCK, PACK], BF16)
            nc.vector.tensor_tensor(
                out=flat(hits01[:]), in0=hit_of[s, 0], in1=hit_of[s, 1], op=ALU.add
            )
            hits01_of[s] = hits01

        def count_all(s):
            if not live(s):
                return
            tied = once.tile([P, BLOCK, PACK], BF16)
            nc.vector.tensor_tensor(
                out=flat(tied[:]), in0=flat(hits01_of[s][:]), in1=hit_of[s, 2], op=ALU.add
            )
            tie_square = pairs2.tile([P, SLAB_COLS], F32)
            nc.scalar.activation(
                out=tie_square[:],
                in_=flat(tied[:]),
                func=ACT.Square,
                bias=TIE_SHIFT,
                scale=TIE_SLOPE,
            )
            tie_square_of[s] = tie_square

        def negate_top(s):
            if not live(s):
                return
            neg_top = thrice.tile(PAIR_SHAPE, F32)
            nc.scalar.activation(out=neg_top[:], in_=top_of[s][:], func=ACT.Copy, scale=-1.0)
            neg_top_of[s] = neg_top

        def find_hit_turned(s, f, bank):
            if not live(s):
                return
            if bank == 0:
                hit_t = turned.tile([P, SLAB_COLS], BF16)
                hit_t_of[s, f] = hit_t
            gap_t = psum_gap.tile([P, BANK], F32, tag="turn")
            for turn in range(TURNS_A_BANK):
                cols = slice(bank * BANK + turn * P, bank * BANK + (turn + 1) * P)
                here = gap_t[:, turn * P : (turn + 1) * P]
                nc.tensor.matmul(
                    out=here,
                    lhsT=line(glu_of[s][:, f])[:, cols],
                    rhs=ident_f32[:],
                    is_transpose=True,
                    start=True,
                    stop=False,
                )
                nc.tensor.matmul(
                    out=here,
                    lhsT=line(neg_top_of[s][:])[:, cols],
                    rhs=ident_f32[:],
                    is_transpose=True,
                    start=False,
                    stop=True,
                )
            nc.scalar.activation(
                out=hit_t_of[s, f][:, bank * BANK : (bank + 1) * BANK],
                in_=gap_t[:],
                func=ACT.Relu,
                bias=1.0,
                scale=GAP_SCALE,
            )

        def count_turning_back(s, bank):
            if not live(s):
                return
            if bank == 0:
                tie_square = pairs2.tile([P, SLAB_COLS], F32)
                tie_square_of[s] = tie_square
            count = psum_gap.tile([P, BANK], F32, tag="turn")
            for turn in range(TURNS_A_BANK):
                cols = slice(bank * BANK + turn * P, bank * BANK + (turn + 1) * P)
                for f in range(BRANCHES):
                    nc.tensor.matmul(
                        out=count[:, turn * P : (turn + 1) * P],
                        lhsT=hit_t_of[s, f][:, cols],
                        rhs=pairs_to_words[:],
                        start=(f == 0),
                        stop=(f == BRANCHES - 1),
                    )
            nc.scalar.activation(
                out=tie_square_of[s][:, bank * BANK : (bank + 1) * BANK],
                in_=count[:],
                func=ACT.Square,
                bias=TIE_SHIFT,
                scale=TIE_SLOPE,
            )

        def turn_hit(s, f):
            if not live(s):
                return
            turning = psum_gap.tile([P, BANK], F32, tag="turn")
            for turn in range(TURNS_A_BANK):
                cols = slice(turn * P, (turn + 1) * P)
                nc.tensor.transpose(
                    turning[:, cols], hit_of[s, f].bitcast(F32)[:, cols], ident_f32[:]
                )
            hit_words = turned.tile([P, BANK], F32, tag="hit_t")
            nc.scalar.copy(out=hit_words[:], in_=turning[:])
            hit_t_of[s, f] = hit_words

        def turn_hit_back(s, f):
            if not live(s):
                return
            hit_back = psum_hit.tile([P, SLAB_COLS], BF16)
            if s == on_vector:
                words_back = hit_back[:].bitcast(F32)
                for turn in range(TURNS_A_BANK):
                    cols = slice(turn * P, (turn + 1) * P)
                    nc.tensor.transpose(
                        words_back[:, cols], hit_t_of[s, f][:, cols], ident_f32[:]
                    )
            else:
                for turn in range(TURNS_A_SLAB):
                    cols = slice(turn * P, (turn + 1) * P)
                    nc.tensor.transpose(
                        hit_back[:, cols], hit_t_of[s, f][:, cols], pairs_to_words[:]
                    )
            hit_of[s, f] = hit_back[:]

        def share_grad(s):
            if not live(s):
                return
            c0 = first_channel(s)
            grad_share = once.tile([P, BLOCK, PACK], F32)
            nc.vector.scalar_tensor_tensor(
                out=flat(grad_share[:]),
                in0=tie_square_of[s][:],
                scalar=TIE_OFFSET,
                in1=flat(grad_words[:, window(s), c0 : c0 + BLOCK, :]),
                op0=ALU.add,
                op1=ALU.mult,
            )
            grad_share_of[s] = grad_share

        def share_grad_times_top(s):
            if not live(s):
                return
            neg_grad_top = once.tile([P, BLOCK, PACK], F32)
            engine = nc.gpsimd if s >= FIRST_ON_GPSIMD else nc.vector
            engine.tensor_tensor(
                out=neg_grad_top[:].rearrange("p (c i) j -> p c i j", i=PAIR),
                in0=grad_share_of[s][:].rearrange("p (c i) j -> p c i j", i=PAIR),
                in1=neg_top_of[s][:].rearrange("p c j i -> p c i j"),
                op=ALU.mult,
            )
            neg_grad_top_of[s] = neg_grad_top

        def dpre(s, f, count):
            if f == 0:
                return dpre_of[s, 0][:]
            return dpre_of[s, 1][:, f - 1 : f - 1 + count]

        def first_half(s, f, count):
            if not live(s):
                return
            if f == 0:
                first_dpre = products_bf16.tile([P, 1, 2, SLAB_COLS], BF16, align_bytes=64)
                dpre_of[s, 0] = first_dpre
            if f == 1:
                other_dpre = products_bf16.tile(
                    [P, BRANCHES - 1, 2, SLAB_COLS], BF16, align_bytes=64
                )
                dpre_of[s, 1] = other_dpre
            nc.vector.tensor_tensor(
                out=dpre(s, f, count)[:, :, 0],
                in0=sg_of[s][:, f : f + count].rearrange("p f c j -> p f (c j)"),
                in1=flat(grad_share_of[s][:]).unsqueeze(1).to_broadcast([P, count, SLAB_COLS]),
                op=ALU.mult,
            )

        def second_half(s, f, count):
            if not live(s):
                return
            nc.vector.scalar_tensor_tensor(
                out=dpre(s, f, count)[:, :, 1],
                in0=sg_of[s][:, f : f + count].rearrange("p f c j -> p f (c j)"),
                scalar=1.0,
                in1=flat(neg_grad_top_of[s][:]).unsqueeze(1).to_broadcast([P, count, SLAB_COLS]),
                op0=ALU.subtract,
                op1=ALU.mult,
            )

        def zero_losers(s, f):
            if not live(s):
                return
            halves = dpre(s, f, 1)[:, 0]
            nc.vector.tensor_tensor(
                out=halves,
                in0=halves,
                in1=hit_of[s, f].unsqueeze(1).to_broadcast([P, 2, SLAB_COLS]),
                op=ALU.mult,
            )

        def quantise(s, f, count):
            if not live(s):
                return
            if f == 0:
                codes = results.tile([P, BRANCHES, N_PASS], U32, align_bytes=64)
                scales = results.tile([P, BRANCHES, N_PASS], U8, align_bytes=64)
                codes_of[s] = codes
                scales_of[s] = scales
            nc.vector.quantize_mx(
                out=codes_of[s][:, f : f + count].rearrange("p f n -> p (f n)").bitcast(E5M2_X4),
                scales=scales_of[s][:, f : f + count].rearrange("p f n -> p (f n)"),
                in_=dpre(s, f, count).rearrange("p f h n -> p (f h n)"),
            )

        def multiply_and_store(s, f, m_tiles):
            if not live(s):
                return
            w, c0 = window(s), first_channel(s)
            for m in m_tiles:
                m_cols = slice(m * M_TILE, (m + 1) * M_TILE)
                closing = s == SLABS - 1 and m % 2 == 1
                if closing:
                    acc = psum_gap.tile([M_TILE, N_PASS], F32, tag="turn")
                else:
                    acc = psum.tile([M_TILE, N_PASS], F32)
                nc.tensor.matmul_mx(
                    out=acc[:],
                    lhsT=agg_codes[:, w, m_cols].bitcast(E4M3_X4),
                    lhsT_scale=agg_scales[:, w, m_cols],
                    rhs=codes_of[s][:, f].bitcast(E5M2_X4),
                    rhs_scale=scales_of[s][:, f],
                    start=True,
                    stop=True,
                )
                result = stage.tile([M_TILE, N_PASS], F32)
                if closing and f == BRANCHES - 1:
                    nc.vector.tensor_copy(out=result[:], in_=acc[:])
                else:
                    nc.scalar.copy(out=result[:], in_=acc[:])
                nc.sync.dma_start(
                    out=out[w, f, m_cols, :].rearrange("p (h c) -> p h c", h=2)[
                        :, :, c0 : c0 + BLOCK
                    ],
                    in_=result[:].rearrange("p (h c) -> p h c", h=2),
                )

        last = BRANCHES - 1

        def turned_path(s):
            return live(s) and s != on_vector

        def convert_and_load(s, f):
            convert(s, f)
            load_rhs(s + 1, f)
            load_lhs(s + 1, f)

        def hit_turned(s, f, bank):
            if turned_path(s):
                find_hit_turned(s, f, bank)

        def count_turned(s, bank):
            if turned_path(s):
                count_turning_back(s, bank)

        def hit_back(s, f):
            if turned_path(s) or (s == on_vector and f > 0):
                turn_hit_back(s, f)

        all_rows = range(M_TILES)
        for f in range(BRANCHES):
            load_rhs(0, f)
            load_lhs(0, f)
        for f in range(BRANCHES):
            convert_and_load(0, f)
        gate_product(0, 0)
        gate_product(0, 1)
        first_max(0)
        gate_product(0, 2)
        second_max(0)
        reorder_grad(0)
        convert_and_load(1, 0)
        negate_top(0)
        convert_and_load(1, 1)
        find_hit(0, 1)
        find_hit(0, 0)
        find_hit(0, 2)
        count_first_two(0)
        count_all(0)
        turn_hit(0, 1)
        turn_hit(0, last)
        turn_hit_back(0, 1)
        turn_hit_back(0, last)
        convert_and_load(1, 2)
        gate_product(1, 0)
        gate_product(1, 1)
        share_grad(0)
        first_max(1)
        gate_product(1, 2)
        share_grad_times_top(0)
        second_max(1)
        convert_and_load(2, 0)
        negate_top(1)
        convert_and_load(2, 1)
        hit_turned(1, 0, 0)
        convert_and_load(2, 2)
        hit_turned(1, 0, 1)
        hit_turned(1, 1, 0)
        reorder_agg(0)
        hit_turned(1, 1, 1)
        for s in range(SLABS + 1):
            nxt = s + 1
            far = s + 2
            final = s == SLABS - 1
            gate_product(far, 0)
            if s > 0:
                share_grad(s)
                share_grad_times_top(s)
            if 0 < s < SLABS:
                zero_losers(s - 1, 1)
                hit_back(s, 0)
                zero_losers(s - 1, last)
                hit_back(s, 1)
            if s == 0:
                first_half(s, 0, 1)
            gate_product(far, 1)
            if s == 0:
                second_half(s, 0, 1)
            if not live(far):
                first_half(s, 0, 1)
            if s < SLABS - 1:
                quantise(s - 1, 1, 2)
            elif final:
                quantise(s - 1, 1, 1)
                quantise(s - 1, last, 1)
            else:
                quantise(s - 1, last, 1)
            first_max(far)
            if s == 0:
                first_half(s, 1, 2)
            gate_product(far, 2)
            if s > 0 and live(far):
                first_half(s, 0, 1)
            if s == 0:
                zero_losers(s, 0)
            second_max(far)
            convert_and_load(far + 1, 0)
            if s == 0:
                hit_turned(nxt, last, 0)
                hit_turned(nxt, last, 1)
                negate_top(far)
                count_turned(nxt, 0)
                count_turned(nxt, 1)
            if s == 1:
                hit_turned(nxt, last, 0)
                hit_turned(nxt, last, 1)
                negate_top(far)
                count_turned(nxt, 0)
                count_turned(nxt, 1)
            if s == 2:
                hit_turned(nxt, last, 0)
                negate_top(far)
            if s > 2:
                hit_turned(nxt, last, 0)
                hit_turned(nxt, last, 1)
                negate_top(far)
                count_turned(nxt, 0)
                count_turned(nxt, 1)
            if s < SLABS:
                multiply_and_store(s - 1, 1, all_rows)
            if s == 2:
                hit_turned(nxt, last, 1)
                count_turned(nxt, 0)
                count_turned(nxt, 1)
            multiply_and_store(s - 1, last, all_rows)
            convert_and_load(far + 1, 1)
            hit_turned(far, 0, 0)
            convert_and_load(far + 1, 2)
            hit_turned(far, 0, 1)
            if s > 0:
                second_half(s, 0, 1)
                first_half(s, 1, 1 if final else 2)
                zero_losers(s, 0)
                hit_back(s, last)
            second_half(s, 1, 1 if final else 2)
            quantise_agg(s)
            quantise(s, 0, 1)
            multiply_and_store(s, 0, range(2))
            hit_turned(far, 1, 0)
            multiply_and_store(s, 0, range(2, 4))
            if s % BLOCKS == 0:
                reorder_agg(s + BLOCKS)
            reorder_grad(far)
            hit_turned(far, 1, 1)
            if final:
                zero_losers(s, 1)
                first_half(s, last, 1)
                quantise(s, 1, 1)
                multiply_and_store(s, 1, all_rows)
                second_half(s, last, 1)
                zero_losers(s, last)
